import numpy as np
import ml_dtypes


def mxq(x, axis, fmt="e4m3"):
    dtype, down = {"e4m3": (ml_dtypes.float8_e4m3fn, 7), "e5m2": (ml_dtypes.float8_e5m2, 14)}[fmt]
    v = np.moveaxis(np.asarray(x, np.float32).astype(ml_dtypes.bfloat16).astype(np.float64), axis, -1)
    blocks = v.reshape(v.shape[:-1] + (-1, 32))
    amax = np.abs(blocks).max(-1, keepdims=True)
    byte = np.maximum(np.where(amax > 0, np.frexp(amax)[1] - 1 + 127, 0) - down, 1)
    scale = np.exp2(byte - 127.0)
    codes = (blocks / scale).astype(np.float32).astype(dtype).astype(np.float64)
    return np.moveaxis((codes * scale).reshape(v.shape), -1, axis)


WIDE = False


def mx_kscale(k):
    if not WIDE:
        return np.ones(k)
    levels = np.array([18, -18])
    if k % 512:
        return np.exp2(np.random.permutation(np.resize(levels, k // 32))).repeat(32)
    a = np.empty((k // 512, 16))
    for p in range(k // 512):
        a[p, :8] = np.random.permutation(np.resize(levels, 8))
        for g in range(8):
            far = levels[np.abs(levels - a[p, g]) >= 10]
            a[p, g + 8] = far[np.random.randint(len(far))]
    return np.exp2(a.ravel()).repeat(32)


BF16 = ml_dtypes.bfloat16


def bf(x):
    return np.asarray(x, np.float32).astype(BF16)


def f64(x):
    return np.asarray(x).astype(np.float64)


B, S, D, F = 2, 256, 1024, 2048


def sigmoid(v):
    return 1.0 / (1.0 + np.exp(-v))


def setup_inputs():
    s = mx_kscale(B * S).reshape(B, S, 1)
    u = mx_kscale(D)
    v = mx_kscale(F)
    x0 = bf(np.random.standard_normal((B, S, D)))
    wg0 = bf(np.random.standard_normal((F, D)) * 1.0 / np.sqrt(D))
    wu0 = bf(np.random.standard_normal((F, D)) * 1.0 / np.sqrt(D))
    wd0 = bf(np.random.standard_normal((D, F)) * 2.0 / np.sqrt(F))
    g = bf(np.random.standard_normal((B, S, D)) * np.exp2(np.random.randint(-6, 1, (B, S, 1))) / s * u)
    xf = f64(x0).reshape(-1, D)
    z_gate = xf @ f64(wg0).T
    z_up = xf @ f64(wu0).T
    return {"x": bf(f64(x0) * s),
            "W_gate": bf(f64(wg0) / v[:, None]),
            "W_up": bf(f64(wu0) / v[:, None]),
            "W_down": bf(f64(wd0) * v[None, :] / u[:, None]),
            "z_gate": np.asarray(z_gate, np.float32),
            "z_up": np.asarray(z_up, np.float32),
            "grad_out": g}


def reference(x, W_gate, W_up, W_down, z_gate, z_up, grad_out):
    x_shape = x.shape
    xf = f64(x).reshape(-1, x_shape[-1])
    g = f64(grad_out).reshape(-1, grad_out.shape[-1])
    zg = f64(z_gate)
    zu = f64(z_up)
    nf = zg.shape[1]
    sg = sigmoid(zg)
    dh = mxq(g, 1, "e5m2") @ mxq(f64(W_down), 0, "e4m3")
    dz_gate = dh * zu * (sg * (1.0 + zg * (1.0 - sg)))
    dz_up = dh * (zg * sg)
    dz1 = np.concatenate([dz_gate, dz_up], axis=1)
    w1 = np.concatenate([f64(W_gate), f64(W_up)], axis=0)
    dx = mxq(dz1, 1, "e5m2") @ mxq(w1, 0, "e4m3")
    dwg = mxq(dz1[:, :nf], 0, "e5m2").T @ mxq(xf, 0, "e4m3")
    return dx.reshape(x_shape), dwg

@@ -1,0 +1,383 @@
+from contextlib import ExitStack
+
+import concourse.mybir as mybir
+from concourse.masks import make_identity
+
+T, D, F = 512, 1024, 2048
+FLOPS = 2 * T * D * F + 2 * T * (2 * F) * D + 2 * F * T * D
+
+F32 = mybir.dt.float32
+BF16 = mybir.dt.bfloat16
+U32 = mybir.dt.uint32
+U8 = mybir.dt.uint8
+E4 = mybir.dt.float8_e4m3fn_x4
+E5 = mybir.dt.float8_e5m2_x4
+ACT = mybir.ActivationFunctionType
+ALU = mybir.AluOpType
+
+P = 128
+CH = 512
+NCH = F // CH
+STEPS = 2 * NCH
+UNITS = 2 * NCH
+
+
+def tile_mixllamamlp_v_kernel(tc, x, W_gate, W_up, W_down, z_gate, z_up, grad_out, out_0, out_1):
+    nc = tc.nc
+    x_v = x.flatten_outer_dims().rearrange("(p j) d -> p j d", j=4)
+    g_v = grad_out.flatten_outer_dims().rearrange("(p j) d -> p j d", j=4)
+    o0_v = out_0.flatten_outer_dims().rearrange("(p j) d -> p j d", j=4)
+    zg_v = z_gate.rearrange("(p j) f -> p j f", j=4)
+    zu_v = z_up.rearrange("(p j) f -> p j f", j=4)
+    wd_v = W_down.rearrange("(k p j) f -> k p j f", p=P, j=4)
+    w_v = [W_gate.rearrange("(c p j) d -> c p j d", p=P, j=4), W_up.rearrange("(c p j) d -> c p j d", p=P, j=4)]
+
+    with ExitStack() as ctx:
+        pool = ctx.enter_context(tc.tile_pool(name="sb", bufs=1))
+        psum = ctx.enter_context(tc.psum_pool(name="ps", bufs=1))
+
+        def sb(tag, shape, dtype, bufs):
+            return pool.tile(shape, dtype, name=tag, tag=tag, bufs=bufs, align_bytes=64)
+
+        def bank(k):
+            return psum.tile([P, 512], F32, name="bank%d" % k, tag="bank%d" % k, bufs=1)
+
+        def grp():
+            return sb("grp", [P, 512, 4], BF16, 9)
+
+        def interleave(copy, dst, src, c0, c1):
+            copy(
+                out=dst[:, c0:c1, :].rearrange("p (c i) t -> p c t i", i=4),
+                in_=src.rearrange("p t (c i) -> p c t i", i=4),
+            )
+
+        def quantize(dst, scales, src, fmt):
+            nc.vector.quantize_mx(out=dst.bitcast(fmt), scales=scales, in_=src[:].rearrange("p c t -> p (c t)"))
+
+        vcopy = nc.vector.tensor_copy
+        scopy = nc.scalar.copy
+
+        ident = sb("ident", [P, P], F32, 1)
+        warm = sb("warm", [P, 1], F32, 1)
+        gc = sb("gc", [P, 2, T], U32, 1)
+        gs = sb("gs", [P, 2, T], U8, 1)
+        xc = sb("xc", [P, D], U32, 1)
+        xs = sb("xs", [P, D], U8, 1)
+        dc = sb("dc", [P, UNITS, T], U32, 1)
+        ds = sb("ds", [P, UNITS, T], U8, 1)
+
+        zg, zu, th, hm = {}, {}, {}, {}
+        wd_raw, wd_grp, wd_c, wd_s = {}, {}, {}, {}
+        w_raw, w_grp, w_c, w_s = {}, {}, {}, {}
+        dzg, dzu, fgrp, tok_grp, tok_c, tok_s = {}, {}, {}, {}, {}, {}
+        dh_bank = {}
+        pending = []
+
+        def load_z(i):
+            c, hp = divmod(i, 2)
+            zg[i] = sb("zg", [P, 2, CH], F32, 4)
+            nc.sync.dma_start(out=zg[i][:], in_=zg_v[:, 2 * hp : 2 * hp + 2, c * CH : (c + 1) * CH])
+            zu[i] = sb("zu", [P, 2, CH], F32, 4)
+            nc.sync.dma_start(out=zu[i][:], in_=zu_v[:, 2 * hp : 2 * hp + 2, c * CH : (c + 1) * CH])
+
+        def load_wd(c, k):
+            wd_raw[c, k] = sb("raw4", [P, 4, CH], BF16, 6)
+            nc.sync.dma_start(out=wd_raw[c, k][:], in_=wd_v[k, :, :, c * CH : (c + 1) * CH])
+
+        def load_w(u):
+            c, which = divmod(u, 2)
+            w_raw[u] = sb("raw8", [P, 4, D], BF16, 3)
+            nc.sync.dma_start(out=w_raw[u][:], in_=w_v[which][c, :, :, :])
+
+        def flush_stores():
+            while pending:
+                dst, st = pending.pop(0)
+                nc.sync.dma_start(out=dst, in_=st)
+
+        def transposes(bk, words, j0, w0):
+            for jj in range(2):
+                for u in range(2):
+                    nc.tensor.transpose(
+                        bk[:, (2 * jj + u) * P : (2 * jj + u + 1) * P],
+                        words[:, j0 + jj, w0 + u : w0 + 256 : 2],
+                        ident[:],
+                    )
+
+        def untranspose_copy(dst, bk, hp):
+            scopy(
+                out=dst[:].bitcast(F32)[:, 256 * hp : 256 * hp + 256, :].rearrange("p (jj r) u -> p jj r u", jj=2),
+                in_=bk[:].rearrange("p (jj u r) -> p jj r u", jj=2, u=2),
+            )
+
+        def wd_int(copy, c, k):
+            wd_grp[c, k] = grp()
+            interleave(copy, wd_grp[c, k], wd_raw[c, k][:], 0, CH)
+
+        def wd_quant(c, k):
+            wd_c[c, k] = sb("wdc", [P, CH], U32, 4)
+            wd_s[c, k] = sb("wds", [P, CH], U8, 4)
+            quantize(wd_c[c, k][:], wd_s[c, k][:], wd_grp[c, k], E4)
+
+        def dh(i):
+            c, hp = divmod(i, 2)
+            for jj in range(2):
+                bk = bank((2 * i + jj) % 4)
+                dh_bank[i, jj] = bk
+                cols = slice((2 * hp + jj) * P, (2 * hp + jj + 1) * P)
+                for k in range(2):
+                    nc.tensor.matmul_mx(
+                        out=bk[:],
+                        lhsT=gc[:, k, cols].bitcast(E5),
+                        lhsT_scale=gs[:, k, cols],
+                        rhs=wd_c[c, k][:].bitcast(E4),
+                        rhs_scale=wd_s[c, k][:],
+                        start=(k == 0),
+                        stop=(k == 1),
+                    )
+
+        def acts_tanh(i):
+            th[i] = sb("th", [P, 2, CH], F32, 3)
+            nc.scalar.activation(out=th[i][:], in_=zg[i][:], func=ACT.Tanh, scale=0.5)
+
+        def acts_silu(i):
+            hm[i] = sb("hm", [P, 2, CH], F32, 3)
+            nc.scalar.activation(out=hm[i][:], in_=zg[i][:], func=ACT.Silu, scale=-1.0)
+
+        def mul_p(i):
+            for jj in range(2):
+                nc.vector.scalar_tensor_tensor(
+                    out=th[i][:, jj, :], in0=th[i][:, jj, :], scalar=1.0, in1=dh_bank[i, jj][:], op0=ALU.add, op1=ALU.mult
+                )
+
+        def mul_up_q(i):
+            dzu[i] = sb("dzu", [P, 2, CH], BF16, 2)
+            nc.vector.scalar_tensor_tensor(
+                out=dzu[i][:], in0=th[i][:], scalar=0.5, in1=zg[i][:], op0=ALU.mult, op1=ALU.mult
+            )
+            nc.vector.scalar_tensor_tensor(
+                out=zu[i][:], in0=th[i][:], scalar=-0.5, in1=zu[i][:], op0=ALU.mult, op1=ALU.mult
+            )
+
+        def mul_gate(i):
+            c, hp = divmod(i, 2)
+            if hp == 0:
+                dzg[c] = sb("dzg", [P, 4, CH], BF16, 2)
+            nc.vector.scalar_tensor_tensor(
+                out=dzg[c][:, 2 * hp : 2 * hp + 2, :], in0=hm[i][:], scalar=1.0, in1=zu[i][:], op0=ALU.subtract, op1=ALU.mult
+            )
+
+        def turn(i):
+            c, hp = divmod(i, 2)
+            if hp == 0:
+                fgrp[2 * c] = grp()
+                fgrp[2 * c + 1] = grp()
+            up = bank(4)
+            transposes(up, dzu[i][:].bitcast(F32), 0, 0)
+            gate = bank(5)
+            transposes(gate, dzg[c][:].bitcast(F32), 2 * hp, 0)
+            untranspose_copy(fgrp[2 * c + 1], up, hp)
+            untranspose_copy(fgrp[2 * c], gate, hp)
+
+        def feat_quant(c):
+            for u in (2 * c, 2 * c + 1):
+                quantize(dc[:, u, :], ds[:, u, :], fgrp[u], E5)
+
+        def tok_int(c):
+            tok_grp[c] = grp()
+            interleave(vcopy, tok_grp[c], dzg[c][:], 0, CH)
+
+        def tok_quant(c):
+            tok_c[c] = sb("tokc", [P, CH], U32, 2)
+            tok_s[c] = sb("toks", [P, CH], U8, 2)
+            quantize(tok_c[c][:], tok_s[c][:], tok_grp[c], E5)
+
+        def dw_half(c, b, half, st):
+            bk = bank(6 + half)
+            cols = slice(b * P, (b + 1) * P)
+            dcols = slice(half * 512, (half + 1) * 512)
+            nc.tensor.matmul_mx(
+                out=bk[:],
+                lhsT=tok_c[c][:, cols].bitcast(E5),
+                lhsT_scale=tok_s[c][:, cols],
+                rhs=xc[:, dcols].bitcast(E4),
+                rhs_scale=xs[:, dcols],
+                start=True,
+                stop=True,
+            )
+            scopy(out=st[:, dcols], in_=bk[:])
+
+        def dw_block(c, b, between=None):
+            st = sb("stage", [P, D], F32, 5)
+            dw_half(c, b, 0, st)
+            if between is not None:
+                between()
+            dw_half(c, b, 1, st)
+            r0 = c * CH + b * P
+            pending.append((out_1[r0 : r0 + P, :], st[:]))
+
+        def w_int_v(u):
+            w_grp[u, 0] = grp()
+            w_grp[u, 1] = grp()
+            interleave(vcopy, w_grp[u, 0], w_raw[u][:, :, 0:512], 0, 512)
+
+        def w_int_s(u):
+            interleave(scopy, w_grp[u, 1], w_raw[u][:, :, 512:1024], 0, 512)
+
+        def w_quant(u, h):
+            if h == 0:
+                w_c[u] = sb("wc", [P, D], U32, 3)
+                w_s[u] = sb("ws", [P, D], U8, 3)
+            cols = slice(h * 512, (h + 1) * 512)
+            quantize(w_c[u][:, cols], w_s[u][:, cols], w_grp[u, h], E4)
+
+        acc = {}
+
+        def dx(u, tiles):
+            for m in tiles:
+                h, j = divmod(m, 4)
+                if u == 0:
+                    acc[m] = bank(m)
+                nc.tensor.matmul_mx(
+                    out=acc[m][:],
+                    lhsT=dc[:, u, j * P : (j + 1) * P].bitcast(E5),
+                    lhsT_scale=ds[:, u, j * P : (j + 1) * P],
+                    rhs=w_c[u][:, h * 512 : (h + 1) * 512].bitcast(E4),
+                    rhs_scale=w_s[u][:, h * 512 : (h + 1) * 512],
+                    start=(u == 0),
+                    stop=(u == UNITS - 1),
+                )
+
+        with tc.manual_schedule():
+            make_identity(nc, ident[:])
+            nc.vector.memset(warm[:], 0.0)
+            nc.scalar.activation(out=warm[:], in_=warm[:], func=ACT.Silu)
+
+            load_wd(0, 0)
+            g_raw = {}
+            for hp in range(2):
+                g_raw[hp] = sb("raw4", [P, 2, D], BF16, 6)
+                nc.sync.dma_start(out=g_raw[hp][:], in_=g_v[:, 2 * hp : 2 * hp + 2, :])
+            load_wd(0, 1)
+            x_raw = sb("raw8", [P, 4, D], BF16, 3)
+            nc.sync.dma_start(out=x_raw[:], in_=x_v)
+            load_z(0)
+            load_wd(1, 0)
+            load_wd(1, 1)
+            load_z(1)
+            load_z(2)
+
+            wd_int(vcopy, 0, 0)
+            g_grp = [grp(), grp()]
+            for hp in range(2):
+                for k in range(2):
+                    bk = bank(4 + k)
+                    transposes(bk, g_raw[hp][:].bitcast(F32), 0, 256 * k)
+                    untranspose_copy(g_grp[k], bk, hp)
+            wd_quant(0, 0)
+            wd_int(vcopy, 0, 1)
+            wd_quant(0, 1)
+            for k in range(2):
+                quantize(gc[:, k, :], gs[:, k, :], g_grp[k], E5)
+            dh(0)
+            acts_tanh(0)
+            acts_silu(0)
+            x_grp = [grp(), grp()]
+            interleave(vcopy, x_grp[0], x_raw[:, :, 0:512], 0, 512)
+            interleave(scopy, x_grp[1], x_raw[:, :, 512:1024], 0, 512)
+            for h in range(2):
+                quantize(xc[:, 512 * h : 512 * h + 512], xs[:, 512 * h : 512 * h + 512], x_grp[h], E4)
+
+            for i in range(STEPS):
+                c, hp = divmod(i, 2)
+                flush_stores()
+                if i + 3 < STEPS:
+                    load_z(i + 3)
+                if hp == 0 and c + 2 < NCH:
+                    load_wd(c + 2, 0)
+                    load_wd(c + 2, 1)
+                if i in (1, 2, 3):
+                    load_w(i - 1)
+                if i > 0:
+                    turn(i - 1)
+                dw = [(c - 1, 0), (c - 1, 1)] if hp == 1 else [(c - 2, 2), (c - 2, 3)]
+                nxt = i + 1 if i + 1 < STEPS else None
+                first = (lambda n=nxt: acts_tanh(n)) if nxt is not None else None
+                second = (lambda n=nxt: acts_silu(n)) if nxt is not None else None
+                if hp == 0 and c + 1 < NCH:
+                    wd_int(scopy, c + 1, 0)
+                if dw[0][0] >= 0:
+                    dw_block(dw[0][0], dw[0][1], first)
+                    dw_block(dw[1][0], dw[1][1], second)
+                elif nxt is not None:
+                    first()
+                    second()
+
+                mul_p(i)
+                if hp == 0:
+                    if c > 0:
+                        tok_int(c - 1)
+                elif c + 1 < NCH:
+                    wd_quant(c + 1, 0)
+                mul_up_q(i)
+                if hp == 0:
+                    if c + 1 < NCH:
+                        wd_int(vcopy, c + 1, 1)
+                elif c + 1 < NCH:
+                    wd_quant(c + 1, 1)
+                if nxt is not None:
+                    dh(nxt)
+                mul_gate(i)
+                if c > 0:
+                    if hp == 0:
+                        tok_quant(c - 1)
+                    else:
+                        feat_quant(c - 1)
+
+            flush_stores()
+            last = NCH - 1
+            turn(STEPS - 1)
+            w_int_v(0)
+            w_int_s(0)
+            load_w(3)
+            tok_int(last)
+            dw_block(last - 1, 2)
+            dw_block(last - 1, 3)
+            flush_stores()
+            w_quant(0, 0)
+            dx(0, range(4))
+            tok_quant(last)
+            w_int_v(1)
+            w_int_s(1)
+            load_w(4)
+            w_quant(0, 1)
+            dw_block(last, 0)
+            dx(0, range(4, 6))
+            dw_block(last, 1)
+            flush_stores()
+            w_quant(1, 0)
+            w_int_v(2)
+            w_int_s(2)
+            load_w(5)
+            w_quant(1, 1)
+            dx(1, range(6))
+            feat_quant(last)
+            dw_block(last, 2)
+            dw_block(last, 3)
+            flush_stores()
+            dx(0, range(6, 8))
+            dx(1, range(6, 8))
+            for u in range(2, UNITS):
+                w_quant(u, 0)
+                if u + 1 < UNITS:
+                    w_int_v(u + 1)
+                    w_int_s(u + 1)
+                    if u + 4 < UNITS:
+                        load_w(u + 4)
+                w_quant(u, 1)
+                dx(u, range(8))
+            for h in range(2):
+                for jp in range(2):
+                    st = sb("stage", [P, 2, 512], F32, 5)
+                    vcopy(out=st[:, 0, :], in_=acc[4 * h + 2 * jp][:])
+                    scopy(out=st[:, 1, :], in_=acc[4 * h + 2 * jp + 1][:])
+                    nc.sync.dma_start(out=o0_v[:, 2 * jp : 2 * jp + 2, 512 * h : 512 * h + 512], in_=st[:])

@@ -20,6 +20,7 @@ CH = 512
 NCH = F // CH
 STEPS = 2 * NCH
 UNITS = 2 * NCH
+DX_BANK = (0, 1, 2, 3, 4, 6, 0, 1)
 
 
 def tile_mixllamamlp_v_kernel(tc, x, W_gate, W_up, W_down, z_gate, z_up, grad_out, out_0, out_1):
@@ -43,7 +44,7 @@ def tile_mixllamamlp_v_kernel(tc, x, W_gate, W_up, W_down, z_gate, z_up, grad_ou
             return psum.tile([P, 512], F32, name="bank%d" % k, tag="bank%d" % k, bufs=1)
 
         def grp():
-            return sb("grp", [P, 512, 4], BF16, 9)
+            return sb("grp", [P, 512, 4], BF16, 11)
 
         def interleave(copy, dst, src, c0, c1):
             copy(
@@ -81,13 +82,13 @@ def tile_mixllamamlp_v_kernel(tc, x, W_gate, W_up, W_down, z_gate, z_up, grad_ou
             nc.sync.dma_start(out=zu[i][:], in_=zu_v[:, 2 * hp : 2 * hp + 2, c * CH : (c + 1) * CH])
 
         def load_wd(c, k):
-            wd_raw[c, k] = sb("raw4", [P, 4, CH], BF16, 6)
+            wd_raw[c, k] = sb("raw4", [P, 4, CH], BF16, 10)
             nc.sync.dma_start(out=wd_raw[c, k][:], in_=wd_v[k, :, :, c * CH : (c + 1) * CH])
 
-        def load_w(u):
+        def load_w(u, h):
             c, which = divmod(u, 2)
-            w_raw[u] = sb("raw8", [P, 4, D], BF16, 3)
-            nc.sync.dma_start(out=w_raw[u][:], in_=w_v[which][c, :, :, :])
+            w_raw[u, h] = sb("raw4", [P, 4, 512], BF16, 10)
+            nc.sync.dma_start(out=w_raw[u, h][:], in_=w_v[which][c, :, :, 512 * h : 512 * h + 512])
 
         def flush_stores():
             while pending:
@@ -103,37 +104,37 @@ def tile_mixllamamlp_v_kernel(tc, x, W_gate, W_up, W_down, z_gate, z_up, grad_ou
                         ident[:],
                     )
 
-        def untranspose_copy(dst, bk, hp):
-            scopy(
+        def untranspose_copy(dst, bk, hp, copy=None):
+            (copy or scopy)(
                 out=dst[:].bitcast(F32)[:, 256 * hp : 256 * hp + 256, :].rearrange("p (jj r) u -> p jj r u", jj=2),
                 in_=bk[:].rearrange("p (jj u r) -> p jj r u", jj=2, u=2),
             )
 
-        def wd_int(copy, c, k):
-            wd_grp[c, k] = grp()
-            interleave(copy, wd_grp[c, k], wd_raw[c, k][:], 0, CH)
+        def wd_int(copy, c, k, c0, c1):
+            if (c, k) not in wd_grp:
+                wd_grp[c, k] = grp()
+            interleave(copy, wd_grp[c, k], wd_raw[c, k][:, :, c0:c1], c0, c1)
 
         def wd_quant(c, k):
             wd_c[c, k] = sb("wdc", [P, CH], U32, 4)
             wd_s[c, k] = sb("wds", [P, CH], U8, 4)
             quantize(wd_c[c, k][:], wd_s[c, k][:], wd_grp[c, k], E4)
 
-        def dh(i):
+        def dh_j(i, jj):
             c, hp = divmod(i, 2)
-            for jj in range(2):
-                bk = bank((2 * i + jj) % 4)
-                dh_bank[i, jj] = bk
-                cols = slice((2 * hp + jj) * P, (2 * hp + jj + 1) * P)
-                for k in range(2):
-                    nc.tensor.matmul_mx(
-                        out=bk[:],
-                        lhsT=gc[:, k, cols].bitcast(E5),
-                        lhsT_scale=gs[:, k, cols],
-                        rhs=wd_c[c, k][:].bitcast(E4),
-                        rhs_scale=wd_s[c, k][:],
-                        start=(k == 0),
-                        stop=(k == 1),
-                    )
+            bk = bank(5 if jj == 1 and i < 3 else 4)
+            dh_bank[i, jj] = bk
+            cols = slice((2 * hp + jj) * P, (2 * hp + jj + 1) * P)
+            for k in range(2):
+                nc.tensor.matmul_mx(
+                    out=bk[:],
+                    lhsT=gc[:, k, cols].bitcast(E5),
+                    lhsT_scale=gs[:, k, cols],
+                    rhs=wd_c[c, k][:].bitcast(E4),
+                    rhs_scale=wd_s[c, k][:],
+                    start=(k == 0),
+                    stop=(k == 1),
+                )
 
         def acts_tanh(i):
             th[i] = sb("th", [P, 2, CH], F32, 3)
@@ -143,17 +144,18 @@ def tile_mixllamamlp_v_kernel(tc, x, W_gate, W_up, W_down, z_gate, z_up, grad_ou
             hm[i] = sb("hm", [P, 2, CH], F32, 3)
             nc.scalar.activation(out=hm[i][:], in_=zg[i][:], func=ACT.Silu, scale=-1.0)
 
-        def mul_p(i):
-            for jj in range(2):
-                nc.vector.scalar_tensor_tensor(
-                    out=th[i][:, jj, :], in0=th[i][:, jj, :], scalar=1.0, in1=dh_bank[i, jj][:], op0=ALU.add, op1=ALU.mult
-                )
+        def mul_p(i, jj):
+            nc.vector.scalar_tensor_tensor(
+                out=th[i][:, jj, :], in0=th[i][:, jj, :], scalar=1.0, in1=dh_bank[i, jj][:], op0=ALU.add, op1=ALU.mult
+            )
 
-        def mul_up_q(i):
+        def mul_up(i):
             dzu[i] = sb("dzu", [P, 2, CH], BF16, 2)
             nc.vector.scalar_tensor_tensor(
                 out=dzu[i][:], in0=th[i][:], scalar=0.5, in1=zg[i][:], op0=ALU.mult, op1=ALU.mult
             )
+
+        def mul_q(i):
             nc.vector.scalar_tensor_tensor(
                 out=zu[i][:], in0=th[i][:], scalar=-0.5, in1=zu[i][:], op0=ALU.mult, op1=ALU.mult
             )
@@ -166,21 +168,23 @@ def tile_mixllamamlp_v_kernel(tc, x, W_gate, W_up, W_down, z_gate, z_up, grad_ou
                 out=dzg[c][:, 2 * hp : 2 * hp + 2, :], in0=hm[i][:], scalar=1.0, in1=zu[i][:], op0=ALU.subtract, op1=ALU.mult
             )
 
-        def turn(i):
-            c, hp = divmod(i, 2)
-            if hp == 0:
-                fgrp[2 * c] = grp()
-                fgrp[2 * c + 1] = grp()
-            up = bank(4)
-            transposes(up, dzu[i][:].bitcast(F32), 0, 0)
-            gate = bank(5)
-            transposes(gate, dzg[c][:].bitcast(F32), 2 * hp, 0)
-            untranspose_copy(fgrp[2 * c + 1], up, hp)
-            untranspose_copy(fgrp[2 * c], gate, hp)
+        tr_bank = {}
 
-        def feat_quant(c):
-            for u in (2 * c, 2 * c + 1):
-                quantize(dc[:, u, :], ds[:, u, :], fgrp[u], E5)
+        def turn_pe(i, gate):
+            c, hp = divmod(i, 2)
+            tr_bank[i, gate] = bank(6)
+            src = dzg[c] if gate else dzu[i]
+            transposes(tr_bank[i, gate], src[:].bitcast(F32), 2 * hp if gate else 0, 0)
+
+        def turn_copy(i, gate):
+            c, hp = divmod(i, 2)
+            u = 2 * c + (0 if gate else 1)
+            if hp == 0:
+                fgrp[u] = grp()
+            untranspose_copy(fgrp[u], tr_bank[i, gate], hp)
+
+        def feat_quant(u):
+            quantize(dc[:, u, :], ds[:, u, :], fgrp[u], E5)
 
         def tok_int(c):
             tok_grp[c] = grp()
@@ -191,12 +195,17 @@ def tile_mixllamamlp_v_kernel(tc, x, W_gate, W_up, W_down, z_gate, z_up, grad_ou
             tok_s[c] = sb("toks", [P, CH], U8, 2)
             quantize(tok_c[c][:], tok_s[c][:], tok_grp[c], E5)
 
-        def dw_half(c, b, half, st):
-            bk = bank(6 + half)
+        stages = {}
+
+        dw_bank = {}
+
+        def dw_pe(n):
+            c, b, half = n
+            dw_bank[n] = bank((5, 7)[half])
             cols = slice(b * P, (b + 1) * P)
             dcols = slice(half * 512, (half + 1) * 512)
             nc.tensor.matmul_mx(
-                out=bk[:],
+                out=dw_bank[n][:],
                 lhsT=tok_c[c][:, cols].bitcast(E5),
                 lhsT_scale=tok_s[c][:, cols],
                 rhs=xc[:, dcols].bitcast(E4),
@@ -204,31 +213,28 @@ def tile_mixllamamlp_v_kernel(tc, x, W_gate, W_up, W_down, z_gate, z_up, grad_ou
                 start=True,
                 stop=True,
             )
-            scopy(out=st[:, dcols], in_=bk[:])
 
-        def dw_block(c, b, between=None):
-            st = sb("stage", [P, D], F32, 5)
-            dw_half(c, b, 0, st)
-            if between is not None:
-                between()
-            dw_half(c, b, 1, st)
-            r0 = c * CH + b * P
-            pending.append((out_1[r0 : r0 + P, :], st[:]))
+        def dw_copy(n, copy=None):
+            c, b, half = n
+            if half == 0:
+                stages[c, b] = sb("stage", [P, D], F32, 5)
+            st = stages[c, b]
+            (copy or scopy)(out=st[:, half * 512 : (half + 1) * 512], in_=dw_bank[n][:])
+            if half == 1:
+                r0 = c * CH + b * P
+                pending.append((out_1[r0 : r0 + P, :], st[:]))
 
-        def w_int_v(u):
-            w_grp[u, 0] = grp()
-            w_grp[u, 1] = grp()
-            interleave(vcopy, w_grp[u, 0], w_raw[u][:, :, 0:512], 0, 512)
-
-        def w_int_s(u):
-            interleave(scopy, w_grp[u, 1], w_raw[u][:, :, 512:1024], 0, 512)
+        def w_int(copy, u, h, c0, c1):
+            if c0 == c1:
+                return
+            if (u, h) not in w_grp:
+                w_grp[u, h] = grp()
+            interleave(copy, w_grp[u, h], w_raw[u, h][:, :, c0:c1], c0, c1)
 
         def w_quant(u, h):
-            if h == 0:
-                w_c[u] = sb("wc", [P, D], U32, 3)
-                w_s[u] = sb("ws", [P, D], U8, 3)
-            cols = slice(h * 512, (h + 1) * 512)
-            quantize(w_c[u][:, cols], w_s[u][:, cols], w_grp[u, h], E4)
+            w_c[u, h] = sb("wc", [P, 512], U32, 5)
+            w_s[u, h] = sb("ws", [P, 512], U8, 5)
+            quantize(w_c[u, h][:], w_s[u, h][:], w_grp[u, h], E4)
 
         acc = {}
 
@@ -236,148 +242,205 @@ def tile_mixllamamlp_v_kernel(tc, x, W_gate, W_up, W_down, z_gate, z_up, grad_ou
             for m in tiles:
                 h, j = divmod(m, 4)
                 if u == 0:
-                    acc[m] = bank(m)
+                    acc[m] = bank(DX_BANK[m])
                 nc.tensor.matmul_mx(
                     out=acc[m][:],
                     lhsT=dc[:, u, j * P : (j + 1) * P].bitcast(E5),
                     lhsT_scale=ds[:, u, j * P : (j + 1) * P],
-                    rhs=w_c[u][:, h * 512 : (h + 1) * 512].bitcast(E4),
-                    rhs_scale=w_s[u][:, h * 512 : (h + 1) * 512],
+                    rhs=w_c[u, h][:].bitcast(E4),
+                    rhs_scale=w_s[u, h][:],
                     start=(u == 0),
                     stop=(u == UNITS - 1),
                 )
 
-        with tc.manual_schedule():
+        def dx_out(copy, m):
+            h, j = divmod(m, 4)
+            if j % 2 == 0:
+                stages["dx", m] = sb("stage", [P, 2, 512], F32, 5)
+            st = stages["dx", m - j % 2]
+            copy(out=st[:, j % 2, :], in_=acc[m][:])
+            nc.sync.dma_start(out=o0_v[:, j, 512 * h : 512 * h + 512], in_=st[:, j % 2, :])
+
+        with tc.manual_schedule(engines={mybir.EngineType.DVE, mybir.EngineType.Activation, mybir.EngineType.SP}):
             make_identity(nc, ident[:])
             nc.vector.memset(warm[:], 0.0)
             nc.scalar.activation(out=warm[:], in_=warm[:], func=ACT.Silu)
 
-            load_wd(0, 0)
             g_raw = {}
+            load_wd(0, 0)
             for hp in range(2):
-                g_raw[hp] = sb("raw4", [P, 2, D], BF16, 6)
+                g_raw[hp] = sb("raw4", [P, 2, D], BF16, 10)
                 nc.sync.dma_start(out=g_raw[hp][:], in_=g_v[:, 2 * hp : 2 * hp + 2, :])
             load_wd(0, 1)
-            x_raw = sb("raw8", [P, 4, D], BF16, 3)
-            nc.sync.dma_start(out=x_raw[:], in_=x_v)
             load_z(0)
+            load_z(1)
             load_wd(1, 0)
             load_wd(1, 1)
-            load_z(1)
+            x_raw = {}
+            for h in range(2):
+                x_raw[h] = sb("raw4", [P, 4, 512], BF16, 10)
+                nc.sync.dma_start(out=x_raw[h][:], in_=x_v[:, :, 512 * h : 512 * h + 512])
             load_z(2)
 
-            wd_int(vcopy, 0, 0)
+            wd_int(vcopy, 0, 0, 0, 512)
+            wd_quant(0, 0)
             g_grp = [grp(), grp()]
             for hp in range(2):
                 for k in range(2):
-                    bk = bank(4 + k)
+                    bk = bank(4 + 2 * k)
                     transposes(bk, g_raw[hp][:].bitcast(F32), 0, 256 * k)
-                    untranspose_copy(g_grp[k], bk, hp)
-            wd_quant(0, 0)
-            wd_int(vcopy, 0, 1)
-            wd_quant(0, 1)
+                    untranspose_copy(g_grp[k], bk, hp, (scopy, vcopy)[k])
+            wd_int(vcopy, 0, 1, 0, 320)
+            wd_int(scopy, 0, 1, 320, 512)
             for k in range(2):
                 quantize(gc[:, k, :], gs[:, k, :], g_grp[k], E5)
-            dh(0)
+            wd_quant(0, 1)
+            dh_j(0, 0)
             acts_tanh(0)
             acts_silu(0)
             x_grp = [grp(), grp()]
-            interleave(vcopy, x_grp[0], x_raw[:, :, 0:512], 0, 512)
-            interleave(scopy, x_grp[1], x_raw[:, :, 512:1024], 0, 512)
-            for h in range(2):
-                quantize(xc[:, 512 * h : 512 * h + 512], xs[:, 512 * h : 512 * h + 512], x_grp[h], E4)
 
             for i in range(STEPS):
                 c, hp = divmod(i, 2)
-                flush_stores()
-                if i + 3 < STEPS:
-                    load_z(i + 3)
+                more = i + 1 < STEPS
+                if i > 0 and i + 2 < STEPS:
+                    load_z(i + 2)
+                load_w(i, 0)
                 if hp == 0 and c + 2 < NCH:
                     load_wd(c + 2, 0)
                     load_wd(c + 2, 1)
-                if i in (1, 2, 3):
-                    load_w(i - 1)
+                if i >= 4:
+                    load_w(i - 4, 1)
+                flush_stores()
+
+                dws = [(c - 1, b, h) for b in range(3) for h in range(2)] if hp == 1 else [(c - 2, 3, 0), (c - 2, 3, 1)]
+                if dws[0][0] < 0:
+                    dws = []
+                vs = (0, 0, 0, 128, 128, 128, 128, 128)[i]
+
+                for n in dws[0:2]:
+                    dw_pe(n)
                 if i > 0:
-                    turn(i - 1)
-                dw = [(c - 1, 0), (c - 1, 1)] if hp == 1 else [(c - 2, 2), (c - 2, 3)]
-                nxt = i + 1 if i + 1 < STEPS else None
-                first = (lambda n=nxt: acts_tanh(n)) if nxt is not None else None
-                second = (lambda n=nxt: acts_silu(n)) if nxt is not None else None
+                    turn_pe(i - 1, True)
+                mul_p(i, 0)
+                dh_j(i, 1)
+                for n in dws[0:1]:
+                    dw_copy(n)
+                if more:
+                    acts_tanh(i + 1)
+                if i > 0:
+                    turn_copy(i - 1, True)
+                for n in dws[1:2]:
+                    dw_copy(n)
+                for n in dws[2:4]:
+                    dw_pe(n)
+                if hp == 0 and c > 0:
+                    tok_int(c - 1)
+                if hp == 1 and c > 0:
+                    feat_quant(2 * c - 1)
+                if i == 2:
+                    for h in range(2):
+                        quantize(xc[:, 512 * h : 512 * h + 512], xs[:, 512 * h : 512 * h + 512], x_grp[h], E4)
+                if i >= 3:
+                    w_quant(i - 3, 0)
                 if hp == 0 and c + 1 < NCH:
-                    wd_int(scopy, c + 1, 0)
-                if dw[0][0] >= 0:
-                    dw_block(dw[0][0], dw[0][1], first)
-                    dw_block(dw[1][0], dw[1][1], second)
-                elif nxt is not None:
-                    first()
-                    second()
-
-                mul_p(i)
-                if hp == 0:
-                    if c > 0:
-                        tok_int(c - 1)
-                elif c + 1 < NCH:
+                    wd_int(scopy, c + 1, 0, 0, 512)
+                mul_p(i, 1)
+                for n in dws[2:3]:
+                    dw_copy(n)
+                if hp == 1 and c + 1 < NCH:
                     wd_quant(c + 1, 0)
-                mul_up_q(i)
-                if hp == 0:
-                    if c + 1 < NCH:
-                        wd_int(vcopy, c + 1, 1)
-                elif c + 1 < NCH:
+                if more:
+                    acts_silu(i + 1)
+                mul_up(i)
+                for n in dws[3:4]:
+                    dw_copy(n)
+                for n in dws[4:6]:
+                    dw_pe(n)
+                if i >= 2:
+                    w_int(scopy, i - 2, 0, vs, 512)
+                turn_pe(i, False)
+                mul_q(i)
+                for n in dws[4:5]:
+                    dw_copy(n)
+                turn_copy(i, False)
+                for n in dws[5:6]:
+                    dw_copy(n)
+                if hp == 0 and c > 0:
+                    tok_quant(c - 1)
+                if hp == 1 and c + 1 < NCH:
                     wd_quant(c + 1, 1)
-                if nxt is not None:
-                    dh(nxt)
+                if more:
+                    dh_j(i + 1, 0)
+                if i >= 4:
+                    dx(i - 4, range(4))
                 mul_gate(i)
-                if c > 0:
-                    if hp == 0:
-                        tok_quant(c - 1)
-                    else:
-                        feat_quant(c - 1)
-
-            flush_stores()
+                if hp == 0 and c + 1 < NCH:
+                    wd_int(vcopy, c + 1, 1, 0, 512)
+                if hp == 1 and c > 0:
+                    feat_quant(2 * c - 2)
+                if i >= 2:
+                    w_int(vcopy, i - 2, 0, 0, vs)
+                if i == 1:
+                    interleave(vcopy, x_grp[0], x_raw[0][:], 0, 512)
+                    interleave(scopy, x_grp[1], x_raw[1][:], 0, 512)
             last = NCH - 1
-            turn(STEPS - 1)
-            w_int_v(0)
-            w_int_s(0)
-            load_w(3)
+            flush_stores()
+            for u in range(4, UNITS):
+                load_w(u, 1)
+            dwl = [(last - 1, 3, h) for h in range(2)] + [(last, b, h) for b in range(4) for h in range(2)]
+            dw_pe(dwl[0])
+            dw_pe(dwl[1])
+            turn_pe(STEPS - 1, True)
+            dx(4, range(4))
+            w_quant(5, 0)
+            dw_copy(dwl[0])
             tok_int(last)
-            dw_block(last - 1, 2)
-            dw_block(last - 1, 3)
+            w_int(vcopy, 6, 0, 0, 256)
+            w_int(scopy, 6, 0, 256, 512)
+            turn_copy(STEPS - 1, True)
+            dw_copy(dwl[1])
             flush_stores()
-            w_quant(0, 0)
-            dx(0, range(4))
             tok_quant(last)
-            w_int_v(1)
-            w_int_s(1)
-            load_w(4)
+            dx(5, range(4))
+            w_int(vcopy, 7, 0, 0, 256)
+            w_int(scopy, 7, 0, 256, 512)
+            dw_pe(dwl[2])
+            dw_pe(dwl[3])
+            feat_quant(7)
+            feat_quant(6)
+            w_quant(6, 0)
+            dx(6, range(4))
+            w_int(scopy, 0, 1, 256, 512)
+            dw_copy(dwl[2])
+            w_int(vcopy, 0, 1, 0, 256)
+            w_quant(7, 0)
+            dx(7, range(4))
+            dw_copy(dwl[3])
+            flush_stores()
+            w_int(vcopy, 1, 1, 0, 256)
+            w_int(scopy, 1, 1, 256, 512)
+            dw_pe(dwl[4])
+            dw_pe(dwl[5])
             w_quant(0, 1)
-            dw_block(last, 0)
-            dx(0, range(4, 6))
-            dw_block(last, 1)
-            flush_stores()
-            w_quant(1, 0)
-            w_int_v(2)
-            w_int_s(2)
-            load_w(5)
-            w_quant(1, 1)
-            dx(1, range(6))
-            feat_quant(last)
-            dw_block(last, 2)
-            dw_block(last, 3)
-            flush_stores()
-            dx(0, range(6, 8))
-            dx(1, range(6, 8))
-            for u in range(2, UNITS):
-                w_quant(u, 0)
+            dn = 4
+            for u in range(UNITS):
+                if u + 2 < UNITS:
+                    vs = (320, 320, 320, 320, 320, 320, 0, 0)[u]
+                    w_int(vcopy, u + 2, 1, 0, vs)
+                    w_int(scopy, u + 2, 1, vs, 512)
+                if u < 2:
+                    dx_out(vcopy, 2 * u)
+                if u < 6:
+                    dw_copy(dwl[dn])
+                    if dn + 2 < 10:
+                        dw_pe(dwl[dn + 2])
+                    dn += 1
+                if u < 2:
+                    dx_out(scopy, 2 * u + 1)
+                flush_stores()
                 if u + 1 < UNITS:
-                    w_int_v(u + 1)
-                    w_int_s(u + 1)
-                    if u + 4 < UNITS:
-                        load_w(u + 4)
-                w_quant(u, 1)
-                dx(u, range(8))
-            for h in range(2):
-                for jp in range(2):
-                    st = sb("stage", [P, 2, 512], F32, 5)
-                    vcopy(out=st[:, 0, :], in_=acc[4 * h + 2 * jp][:])
-                    scopy(out=st[:, 1, :], in_=acc[4 * h + 2 * jp + 1][:])
-                    nc.sync.dma_start(out=o0_v[:, 2 * jp : 2 * jp + 2, 512 * h : 512 * h + 512], in_=st[:])
+                    w_quant(u + 1, 1)
+                dx(u, range(4, 8))
+            for m in range(4, 8):
+                dx_out((vcopy, scopy)[m % 2], m)

@@ -10,437 +10,471 @@ F32 = mybir.dt.float32
 BF16 = mybir.dt.bfloat16
 U32 = mybir.dt.uint32
 U8 = mybir.dt.uint8
-E4 = mybir.dt.float8_e4m3fn_x4
-E5 = mybir.dt.float8_e5m2_x4
+E4M3 = mybir.dt.float8_e4m3fn_x4
+E5M2 = mybir.dt.float8_e5m2_x4
 ACT = mybir.ActivationFunctionType
 ALU = mybir.AluOpType
+ENGINE = mybir.EngineType
 
 P = 128
-CH = 512
-NCH = F // CH
-STEPS = 2 * NCH
-UNITS = 2 * NCH
+SLOTS = 4
+PASS = P * SLOTS
+N = 512
+CHUNKS = F // PASS
+STEPS = 2 * CHUNKS
+UNITS = 2 * CHUNKS
+
 DX_BANK = (0, 1, 2, 3, 4, 6, 0, 1)
+DH_BANK = 4
+TURN_BANK = 6
+DW_BANKS = (5, 7)
+DW_FIRST_STEP = 3
+
+V_COLS_W = (
+    (0, 128, 128, 128, 128, 128, 256, 256),
+    (256, 256, 384, 384, 384, 320, 320, 256),
+)
+V_COLS_WD_HEAD = 192
+V_COLS_WD_NEXT = 256
 
 
 def tile_mixllamamlp_v_kernel(tc, x, W_gate, W_up, W_down, z_gate, z_up, grad_out, out_0, out_1):
     nc = tc.nc
-    x_v = x.flatten_outer_dims().rearrange("(p j) d -> p j d", j=4)
-    g_v = grad_out.flatten_outer_dims().rearrange("(p j) d -> p j d", j=4)
-    o0_v = out_0.flatten_outer_dims().rearrange("(p j) d -> p j d", j=4)
-    zg_v = z_gate.rearrange("(p j) f -> p j f", j=4)
-    zu_v = z_up.rearrange("(p j) f -> p j f", j=4)
-    wd_v = W_down.rearrange("(k p j) f -> k p j f", p=P, j=4)
-    w_v = [W_gate.rearrange("(c p j) d -> c p j d", p=P, j=4), W_up.rearrange("(c p j) d -> c p j d", p=P, j=4)]
+    x_rows = x.flatten_outer_dims().rearrange("(p j) d -> p j d", j=SLOTS)
+    g_rows = grad_out.flatten_outer_dims().rearrange("(p j) d -> p j d", j=SLOTS)
+    dx_rows = out_0.flatten_outer_dims().rearrange("(p j) d -> p j d", j=SLOTS)
+    zg_rows = z_gate.rearrange("(p j) f -> p j f", j=SLOTS)
+    zu_rows = z_up.rearrange("(p j) f -> p j f", j=SLOTS)
+    wd_rows = W_down.rearrange("(k p j) f -> k p j f", p=P, j=SLOTS)
+    w_rows = [w.rearrange("(c p j) d -> c p j d", p=P, j=SLOTS) for w in (W_gate, W_up)]
 
     with ExitStack() as ctx:
         pool = ctx.enter_context(tc.tile_pool(name="sb", bufs=1))
         psum = ctx.enter_context(tc.psum_pool(name="ps", bufs=1))
+        vector_copy = nc.vector.tensor_copy
+        scalar_copy = nc.scalar.copy
 
         def sb(tag, shape, dtype, bufs):
             return pool.tile(shape, dtype, name=tag, tag=tag, bufs=bufs, align_bytes=64)
 
         def bank(k):
-            return psum.tile([P, 512], F32, name="bank%d" % k, tag="bank%d" % k, bufs=1)
+            return psum.tile([P, N], F32, name="bank%d" % k, tag="bank%d" % k, bufs=1)
 
-        def grp():
-            return sb("grp", [P, 512, 4], BF16, 11)
+        def raw_tile(shape):
+            return sb("raw", shape, BF16, 10)
 
-        def interleave(copy, dst, src, c0, c1):
-            copy(
-                out=dst[:, c0:c1, :].rearrange("p (c i) t -> p c t i", i=4),
-                in_=src.rearrange("p t (c i) -> p c t i", i=4),
-            )
+        def grouped_tile():
+            return sb("grouped", [P, N, SLOTS], BF16, 11)
 
-        def quantize(dst, scales, src, fmt):
-            nc.vector.quantize_mx(out=dst.bitcast(fmt), scales=scales, in_=src[:].rearrange("p c t -> p (c t)"))
+        def stage_tile(shape):
+            return sb("stage", shape, F32, 5)
 
-        vcopy = nc.vector.tensor_copy
-        scopy = nc.scalar.copy
-
-        ident = sb("ident", [P, P], F32, 1)
+        identity = sb("identity", [P, P], F32, 1)
         warm = sb("warm", [P, 1], F32, 1)
-        gc = sb("gc", [P, 2, T], U32, 1)
-        gs = sb("gs", [P, 2, T], U8, 1)
-        xc = sb("xc", [P, D], U32, 1)
-        xs = sb("xs", [P, D], U8, 1)
-        dc = sb("dc", [P, UNITS, T], U32, 1)
-        ds = sb("ds", [P, UNITS, T], U8, 1)
+        g_codes = sb("g_codes", [P, 2, T], U32, 1)
+        g_scales = sb("g_scales", [P, 2, T], U8, 1)
+        x_codes = sb("x_codes", [P, D], U32, 1)
+        x_scales = sb("x_scales", [P, D], U8, 1)
+        dz_codes = sb("dz_codes", [P, UNITS, T], U32, 1)
+        dz_scales = sb("dz_scales", [P, UNITS, T], U8, 1)
 
-        zg, zu, th, hm = {}, {}, {}, {}
-        wd_raw, wd_grp, wd_c, wd_s = {}, {}, {}, {}
-        w_raw, w_grp, w_c, w_s = {}, {}, {}, {}
-        dzg, dzu, fgrp, tok_grp, tok_c, tok_s = {}, {}, {}, {}, {}, {}
-        dh_bank = {}
-        pending = []
+        zg, zu, th, sm = {}, {}, {}, {}
+        wd_raw, wd_grouped, wd_codes, wd_scales = {}, {}, {}, {}
+        w_raw, w_grouped, w_codes, w_scales = {}, {}, {}, {}
+        g_raw, x_raw = {}, {}
+        dz_gate, dz_up, dz_grouped = {}, {}, {}
+        tok_grouped, tok_codes, tok_scales = {}, {}, {}
+        dh, turned, dx_sum, dw_sum, stages = {}, {}, {}, {}, {}
+        stores = []
+
+        def load_half_z(tiles, rows, tag, i):
+            c, hp = divmod(i, 2)
+            tiles[i] = sb(tag, [P, 2, PASS], F32, 4)
+            nc.sync.dma_start(out=tiles[i][:], in_=rows[:, 2 * hp : 2 * hp + 2, c * PASS : (c + 1) * PASS])
 
         def load_z(i):
-            c, hp = divmod(i, 2)
-            zg[i] = sb("zg", [P, 2, CH], F32, 4)
-            nc.sync.dma_start(out=zg[i][:], in_=zg_v[:, 2 * hp : 2 * hp + 2, c * CH : (c + 1) * CH])
-            zu[i] = sb("zu", [P, 2, CH], F32, 4)
-            nc.sync.dma_start(out=zu[i][:], in_=zu_v[:, 2 * hp : 2 * hp + 2, c * CH : (c + 1) * CH])
+            load_half_z(zg, zg_rows, "zg", i)
+            load_half_z(zu, zu_rows, "zu", i)
+
+        def load_g(hp):
+            g_raw[hp] = raw_tile([P, 2, D])
+            nc.sync.dma_start(out=g_raw[hp][:], in_=g_rows[:, 2 * hp : 2 * hp + 2, :])
+
+        def load_x(h):
+            x_raw[h] = raw_tile([P, SLOTS, N])
+            nc.sync.dma_start(out=x_raw[h][:], in_=x_rows[:, :, N * h : N * h + N])
 
         def load_wd(c, k):
-            wd_raw[c, k] = sb("raw4", [P, 4, CH], BF16, 10)
-            nc.sync.dma_start(out=wd_raw[c, k][:], in_=wd_v[k, :, :, c * CH : (c + 1) * CH])
+            wd_raw[c, k] = raw_tile([P, SLOTS, PASS])
+            nc.sync.dma_start(out=wd_raw[c, k][:], in_=wd_rows[k, :, :, c * PASS : (c + 1) * PASS])
 
         def load_w(u, h):
-            c, which = divmod(u, 2)
-            w_raw[u, h] = sb("raw4", [P, 4, 512], BF16, 10)
-            nc.sync.dma_start(out=w_raw[u, h][:], in_=w_v[which][c, :, :, 512 * h : 512 * h + 512])
+            w_raw[u, h] = raw_tile([P, SLOTS, N])
+            nc.sync.dma_start(out=w_raw[u, h][:], in_=w_rows[u % 2][u // 2, :, :, N * h : N * h + N])
 
-        def flush_stores():
-            while pending:
-                dst, st = pending.pop(0)
-                nc.sync.dma_start(out=dst, in_=st)
+        def issue_stores():
+            while stores:
+                dst, src = stores.pop(0)
+                nc.sync.dma_start(out=dst, in_=src)
 
-        def transposes(bk, words, j0, w0):
-            for jj in range(2):
-                for u in range(2):
-                    nc.tensor.transpose(
-                        bk[:, (2 * jj + u) * P : (2 * jj + u + 1) * P],
-                        words[:, j0 + jj, w0 + u : w0 + 256 : 2],
-                        ident[:],
-                    )
-
-        def untranspose_copy(dst, bk, hp, copy=None):
-            (copy or scopy)(
-                out=dst[:].bitcast(F32)[:, 256 * hp : 256 * hp + 256, :].rearrange("p (jj r) u -> p jj r u", jj=2),
-                in_=bk[:].rearrange("p (jj u r) -> p jj r u", jj=2, u=2),
+        def group(copy, dst, raw, c0, c1):
+            copy(
+                out=dst[:, c0:c1, :].rearrange("p (c i) t -> p c t i", i=4),
+                in_=raw[:, :, c0:c1].rearrange("p t (c i) -> p c t i", i=4),
             )
 
-        def wd_int(copy, c, k, c0, c1):
-            if (c, k) not in wd_grp:
-                wd_grp[c, k] = grp()
-            interleave(copy, wd_grp[c, k], wd_raw[c, k][:, :, c0:c1], c0, c1)
+        def quantize(codes, scales, grouped, fmt):
+            nc.vector.quantize_mx(out=codes.bitcast(fmt), scales=scales, in_=grouped[:].rearrange("p c t -> p (c t)"))
 
-        def wd_quant(c, k):
-            wd_c[c, k] = sb("wdc", [P, CH], U32, 4)
-            wd_s[c, k] = sb("wds", [P, CH], U8, 4)
-            quantize(wd_c[c, k][:], wd_s[c, k][:], wd_grp[c, k], E4)
+        def group_wd(copy, c, k, c0, c1):
+            if (c, k) not in wd_grouped:
+                wd_grouped[c, k] = grouped_tile()
+            group(copy, wd_grouped[c, k], wd_raw[c, k], c0, c1)
 
-        def dh_j(i, jj):
+        def quantize_wd(c, k):
+            wd_codes[c, k] = sb("wd_codes", [P, PASS], U32, 4)
+            wd_scales[c, k] = sb("wd_scales", [P, PASS], U8, 4)
+            quantize(wd_codes[c, k][:], wd_scales[c, k][:], wd_grouped[c, k], E4M3)
+
+        def group_w(copy, u, h):
+            cut = V_COLS_W[h][u]
+            c0, c1 = (0, cut) if copy is vector_copy else (cut, N)
+            if c0 < c1:
+                if (u, h) not in w_grouped:
+                    w_grouped[u, h] = grouped_tile()
+                group(copy, w_grouped[u, h], w_raw[u, h], c0, c1)
+
+        def quantize_w(u, h):
+            w_codes[u, h] = sb("w_codes", [P, N], U32, 5)
+            w_scales[u, h] = sb("w_scales", [P, N], U8, 5)
+            quantize(w_codes[u, h][:], w_scales[u, h][:], w_grouped[u, h], E4M3)
+
+        def quantize_x(h):
+            cols = slice(N * h, N * h + N)
+            quantize(x_codes[:, cols], x_scales[:, cols], x_grouped[h], E4M3)
+
+        def transpose_words(out, words, j0, w0):
+            for jj in range(2):
+                for u in range(2):
+                    block = 2 * jj + u
+                    nc.tensor.transpose(
+                        out[:, block * P : (block + 1) * P], words[:, j0 + jj, w0 + u : w0 + 256 : 2], identity[:]
+                    )
+
+        def copy_turned(copy, dst, src, hp):
+            copy(
+                out=dst[:].bitcast(F32)[:, 256 * hp : 256 * hp + 256, :].rearrange("p (jj r) u -> p jj r u", jj=2),
+                in_=src[:].rearrange("p (jj u r) -> p jj r u", jj=2, u=2),
+            )
+
+        def turn_dz(i, gate):
             c, hp = divmod(i, 2)
-            bk = bank(5 if jj == 1 and i < 3 else 4)
-            dh_bank[i, jj] = bk
-            cols = slice((2 * hp + jj) * P, (2 * hp + jj + 1) * P)
+            turned[i, gate] = bank(TURN_BANK)
+            if gate:
+                transpose_words(turned[i, gate], dz_gate[c][:].bitcast(F32), 2 * hp, 0)
+            else:
+                transpose_words(turned[i, gate], dz_up[i][:].bitcast(F32), 0, 0)
+
+        def copy_turned_dz(i, gate):
+            c, hp = divmod(i, 2)
+            u = 2 * c if gate else 2 * c + 1
+            if hp == 0:
+                dz_grouped[u] = grouped_tile()
+            copy_turned(scalar_copy, dz_grouped[u], turned[i, gate], hp)
+
+        def quantize_dz(u):
+            quantize(dz_codes[:, u, :], dz_scales[:, u, :], dz_grouped[u], E5M2)
+
+        def dh_slot(i, jj):
+            c, hp = divmod(i, 2)
+            dh[i, jj] = bank(DW_BANKS[0] if jj == 1 and i < DW_FIRST_STEP else DH_BANK)
+            j = 2 * hp + jj
+            cols = slice(j * P, (j + 1) * P)
             for k in range(2):
                 nc.tensor.matmul_mx(
-                    out=bk[:],
-                    lhsT=gc[:, k, cols].bitcast(E5),
-                    lhsT_scale=gs[:, k, cols],
-                    rhs=wd_c[c, k][:].bitcast(E4),
-                    rhs_scale=wd_s[c, k][:],
+                    out=dh[i, jj][:],
+                    lhsT=g_codes[:, k, cols].bitcast(E5M2),
+                    lhsT_scale=g_scales[:, k, cols],
+                    rhs=wd_codes[c, k][:].bitcast(E4M3),
+                    rhs_scale=wd_scales[c, k][:],
                     start=(k == 0),
                     stop=(k == 1),
                 )
 
-        def acts_tanh(i):
-            th[i] = sb("th", [P, 2, CH], F32, 3)
+        def tanh_half(i):
+            th[i] = sb("th", [P, 2, PASS], F32, 3)
             nc.scalar.activation(out=th[i][:], in_=zg[i][:], func=ACT.Tanh, scale=0.5)
 
-        def acts_silu(i):
-            hm[i] = sb("hm", [P, 2, CH], F32, 3)
-            nc.scalar.activation(out=hm[i][:], in_=zg[i][:], func=ACT.Silu, scale=-1.0)
+        def silu_minus(i):
+            sm[i] = sb("sm", [P, 2, PASS], F32, 3)
+            nc.scalar.activation(out=sm[i][:], in_=zg[i][:], func=ACT.Silu, scale=-1.0)
 
-        def mul_p(i, jj):
-            nc.vector.scalar_tensor_tensor(
-                out=th[i][:, jj, :], in0=th[i][:, jj, :], scalar=1.0, in1=dh_bank[i, jj][:], op0=ALU.add, op1=ALU.mult
-            )
+        def times(out, a, scalar, b, op):
+            nc.vector.scalar_tensor_tensor(out=out, in0=a, scalar=scalar, in1=b, op0=op, op1=ALU.mult)
 
-        def mul_up(i):
-            dzu[i] = sb("dzu", [P, 2, CH], BF16, 2)
-            nc.vector.scalar_tensor_tensor(
-                out=dzu[i][:], in0=th[i][:], scalar=0.5, in1=zg[i][:], op0=ALU.mult, op1=ALU.mult
-            )
+        def make_p(i, jj):
+            times(th[i][:, jj, :], th[i][:, jj, :], 1.0, dh[i, jj][:], ALU.add)
 
-        def mul_q(i):
-            nc.vector.scalar_tensor_tensor(
-                out=zu[i][:], in0=th[i][:], scalar=-0.5, in1=zu[i][:], op0=ALU.mult, op1=ALU.mult
-            )
+        def make_dz_up(i):
+            dz_up[i] = sb("dz_up", [P, 2, PASS], BF16, 2)
+            times(dz_up[i][:], th[i][:], 0.5, zg[i][:], ALU.mult)
 
-        def mul_gate(i):
+        def make_q(i):
+            times(zu[i][:], th[i][:], -0.5, zu[i][:], ALU.mult)
+
+        def make_dz_gate(i):
             c, hp = divmod(i, 2)
             if hp == 0:
-                dzg[c] = sb("dzg", [P, 4, CH], BF16, 2)
-            nc.vector.scalar_tensor_tensor(
-                out=dzg[c][:, 2 * hp : 2 * hp + 2, :], in0=hm[i][:], scalar=1.0, in1=zu[i][:], op0=ALU.subtract, op1=ALU.mult
-            )
+                dz_gate[c] = sb("dz_gate", [P, SLOTS, PASS], BF16, 2)
+            times(dz_gate[c][:, 2 * hp : 2 * hp + 2, :], sm[i][:], 1.0, zu[i][:], ALU.subtract)
 
-        tr_bank = {}
+        def group_tokens(c):
+            tok_grouped[c] = grouped_tile()
+            group(vector_copy, tok_grouped[c], dz_gate[c], 0, PASS)
 
-        def turn_pe(i, gate):
-            c, hp = divmod(i, 2)
-            tr_bank[i, gate] = bank(6)
-            src = dzg[c] if gate else dzu[i]
-            transposes(tr_bank[i, gate], src[:].bitcast(F32), 2 * hp if gate else 0, 0)
+        def quantize_tokens(c):
+            tok_codes[c] = sb("tok_codes", [P, PASS], U32, 2)
+            tok_scales[c] = sb("tok_scales", [P, PASS], U8, 2)
+            quantize(tok_codes[c][:], tok_scales[c][:], tok_grouped[c], E5M2)
 
-        def turn_copy(i, gate):
-            c, hp = divmod(i, 2)
-            u = 2 * c + (0 if gate else 1)
-            if hp == 0:
-                fgrp[u] = grp()
-            untranspose_copy(fgrp[u], tr_bank[i, gate], hp)
-
-        def feat_quant(u):
-            quantize(dc[:, u, :], ds[:, u, :], fgrp[u], E5)
-
-        def tok_int(c):
-            tok_grp[c] = grp()
-            interleave(vcopy, tok_grp[c], dzg[c][:], 0, CH)
-
-        def tok_quant(c):
-            tok_c[c] = sb("tokc", [P, CH], U32, 2)
-            tok_s[c] = sb("toks", [P, CH], U8, 2)
-            quantize(tok_c[c][:], tok_s[c][:], tok_grp[c], E5)
-
-        stages = {}
-
-        dw_bank = {}
-
-        def dw_pe(n):
-            c, b, half = n
-            dw_bank[n] = bank((5, 7)[half])
-            cols = slice(b * P, (b + 1) * P)
-            dcols = slice(half * 512, (half + 1) * 512)
+        def dw(n):
+            c, b, h = n
+            dw_sum[n] = bank(DW_BANKS[h])
+            rows, cols = slice(b * P, (b + 1) * P), slice(N * h, N * h + N)
             nc.tensor.matmul_mx(
-                out=dw_bank[n][:],
-                lhsT=tok_c[c][:, cols].bitcast(E5),
-                lhsT_scale=tok_s[c][:, cols],
-                rhs=xc[:, dcols].bitcast(E4),
-                rhs_scale=xs[:, dcols],
+                out=dw_sum[n][:],
+                lhsT=tok_codes[c][:, rows].bitcast(E5M2),
+                lhsT_scale=tok_scales[c][:, rows],
+                rhs=x_codes[:, cols].bitcast(E4M3),
+                rhs_scale=x_scales[:, cols],
                 start=True,
                 stop=True,
             )
 
-        def dw_copy(n, copy=None):
-            c, b, half = n
-            if half == 0:
-                stages[c, b] = sb("stage", [P, D], F32, 5)
-            st = stages[c, b]
-            (copy or scopy)(out=st[:, half * 512 : (half + 1) * 512], in_=dw_bank[n][:])
-            if half == 1:
-                r0 = c * CH + b * P
-                pending.append((out_1[r0 : r0 + P, :], st[:]))
+        def dw_out(n, copy):
+            c, b, h = n
+            if h == 0:
+                stages[c, b] = stage_tile([P, D])
+            copy(out=stages[c, b][:, N * h : N * h + N], in_=dw_sum[n][:])
+            if h == 1:
+                row = c * PASS + b * P
+                stores.append((out_1[row : row + P, :], stages[c, b][:]))
 
-        def w_int(copy, u, h, c0, c1):
-            if c0 == c1:
-                return
-            if (u, h) not in w_grp:
-                w_grp[u, h] = grp()
-            interleave(copy, w_grp[u, h], w_raw[u, h][:, :, c0:c1], c0, c1)
-
-        def w_quant(u, h):
-            w_c[u, h] = sb("wc", [P, 512], U32, 5)
-            w_s[u, h] = sb("ws", [P, 512], U8, 5)
-            quantize(w_c[u, h][:], w_s[u, h][:], w_grp[u, h], E4)
-
-        acc = {}
-
-        def dx(u, tiles):
-            for m in tiles:
-                h, j = divmod(m, 4)
+        def dx(u, h):
+            for j in range(SLOTS):
+                m = SLOTS * h + j
+                cols = slice(j * P, (j + 1) * P)
                 if u == 0:
-                    acc[m] = bank(DX_BANK[m])
+                    dx_sum[m] = bank(DX_BANK[m])
                 nc.tensor.matmul_mx(
-                    out=acc[m][:],
-                    lhsT=dc[:, u, j * P : (j + 1) * P].bitcast(E5),
-                    lhsT_scale=ds[:, u, j * P : (j + 1) * P],
-                    rhs=w_c[u, h][:].bitcast(E4),
-                    rhs_scale=w_s[u, h][:],
+                    out=dx_sum[m][:],
+                    lhsT=dz_codes[:, u, cols].bitcast(E5M2),
+                    lhsT_scale=dz_scales[:, u, cols],
+                    rhs=w_codes[u, h][:].bitcast(E4M3),
+                    rhs_scale=w_scales[u, h][:],
                     start=(u == 0),
                     stop=(u == UNITS - 1),
                 )
 
-        def dx_out(copy, m):
-            h, j = divmod(m, 4)
+        def dx_out(m, copy):
+            h, j = divmod(m, SLOTS)
             if j % 2 == 0:
-                stages["dx", m] = sb("stage", [P, 2, 512], F32, 5)
-            st = stages["dx", m - j % 2]
-            copy(out=st[:, j % 2, :], in_=acc[m][:])
-            nc.sync.dma_start(out=o0_v[:, j, 512 * h : 512 * h + 512], in_=st[:, j % 2, :])
+                stages["dx", m] = stage_tile([P, 2, N])
+            half_stage = stages["dx", m - j % 2][:, j % 2, :]
+            copy(out=half_stage, in_=dx_sum[m][:])
+            nc.sync.dma_start(out=dx_rows[:, j, N * h : N * h + N], in_=half_stage)
 
-        with tc.manual_schedule(engines={mybir.EngineType.DVE, mybir.EngineType.Activation, mybir.EngineType.SP}):
-            make_identity(nc, ident[:])
+        with tc.manual_schedule(engines={ENGINE.DVE, ENGINE.Activation, ENGINE.SP}):
+            make_identity(nc, identity[:])
             nc.vector.memset(warm[:], 0.0)
             nc.scalar.activation(out=warm[:], in_=warm[:], func=ACT.Silu)
 
-            g_raw = {}
             load_wd(0, 0)
-            for hp in range(2):
-                g_raw[hp] = sb("raw4", [P, 2, D], BF16, 10)
-                nc.sync.dma_start(out=g_raw[hp][:], in_=g_v[:, 2 * hp : 2 * hp + 2, :])
+            load_g(0)
+            load_g(1)
             load_wd(0, 1)
-            load_z(0)
+            load_half_z(zg, zg_rows, "zg", 0)
+            load_x(0)
+            load_half_z(zu, zu_rows, "zu", 0)
             load_z(1)
             load_wd(1, 0)
             load_wd(1, 1)
-            x_raw = {}
-            for h in range(2):
-                x_raw[h] = sb("raw4", [P, 4, 512], BF16, 10)
-                nc.sync.dma_start(out=x_raw[h][:], in_=x_v[:, :, 512 * h : 512 * h + 512])
             load_z(2)
+            load_x(1)
 
-            wd_int(vcopy, 0, 0, 0, 512)
-            wd_quant(0, 0)
-            g_grp = [grp(), grp()]
+            group_wd(vector_copy, 0, 0, 0, PASS)
+            quantize_wd(0, 0)
+            g_grouped = [grouped_tile(), grouped_tile()]
             for hp in range(2):
                 for k in range(2):
-                    bk = bank(4 + 2 * k)
-                    transposes(bk, g_raw[hp][:].bitcast(F32), 0, 256 * k)
-                    untranspose_copy(g_grp[k], bk, hp, (scopy, vcopy)[k])
-            wd_int(vcopy, 0, 1, 0, 320)
-            wd_int(scopy, 0, 1, 320, 512)
+                    g_turned = bank((DH_BANK, TURN_BANK)[k])
+                    transpose_words(g_turned, g_raw[hp][:].bitcast(F32), 0, 256 * k)
+                    copy_turned((scalar_copy, vector_copy)[k], g_grouped[k], g_turned, hp)
+            group_wd(vector_copy, 0, 1, 0, V_COLS_WD_HEAD)
+            group_wd(scalar_copy, 0, 1, V_COLS_WD_HEAD, PASS)
             for k in range(2):
-                quantize(gc[:, k, :], gs[:, k, :], g_grp[k], E5)
-            wd_quant(0, 1)
-            dh_j(0, 0)
-            acts_tanh(0)
-            acts_silu(0)
-            x_grp = [grp(), grp()]
+                quantize(g_codes[:, k, :], g_scales[:, k, :], g_grouped[k], E5M2)
+            quantize_wd(0, 1)
+            dh_slot(0, 0)
+            tanh_half(0)
+            silu_minus(0)
+            x_grouped = [grouped_tile(), grouped_tile()]
+            group(vector_copy, x_grouped[0], x_raw[0], 0, N)
 
             for i in range(STEPS):
                 c, hp = divmod(i, 2)
-                more = i + 1 < STEPS
-                if i > 0 and i + 2 < STEPS:
+                next_step = i + 1 < STEPS
+                next_chunk = c + 1 < CHUNKS
+
+                if i == 0:
+                    load_wd(2, 0)
+                    load_wd(2, 1)
+                    load_z(3)
+                if 1 < i and i + 2 < STEPS:
                     load_z(i + 2)
                 load_w(i, 0)
-                if hp == 0 and c + 2 < NCH:
+                if hp == 0 and 0 < c and c + 2 < CHUNKS:
                     load_wd(c + 2, 0)
                     load_wd(c + 2, 1)
                 if i >= 4:
                     load_w(i - 4, 1)
-                flush_stores()
+                issue_stores()
 
-                dws = [(c - 1, b, h) for b in range(3) for h in range(2)] if hp == 1 else [(c - 2, 3, 0), (c - 2, 3, 1)]
-                if dws[0][0] < 0:
-                    dws = []
-                vs = (0, 0, 0, 128, 128, 128, 128, 128)[i]
+                if hp == 1:
+                    blocks = [(c - 1, b, h) for b in range(3) for h in range(2)] if c > 0 else []
+                else:
+                    blocks = [(c - 2, 3, h) for h in range(2)] if c > 1 else []
 
-                for n in dws[0:2]:
-                    dw_pe(n)
+                for n in blocks[0:2]:
+                    dw(n)
                 if i > 0:
-                    turn_pe(i - 1, True)
-                mul_p(i, 0)
-                dh_j(i, 1)
-                for n in dws[0:1]:
-                    dw_copy(n)
-                if more:
-                    acts_tanh(i + 1)
+                    turn_dz(i - 1, True)
+                make_p(i, 0)
+                dh_slot(i, 1)
+                for n in blocks[0:1]:
+                    dw_out(n, scalar_copy)
+                if next_step:
+                    tanh_half(i + 1)
                 if i > 0:
-                    turn_copy(i - 1, True)
-                for n in dws[1:2]:
-                    dw_copy(n)
-                for n in dws[2:4]:
-                    dw_pe(n)
+                    copy_turned_dz(i - 1, True)
+                for n in blocks[1:2]:
+                    dw_out(n, scalar_copy)
+                for n in blocks[2:4]:
+                    dw(n)
                 if hp == 0 and c > 0:
-                    tok_int(c - 1)
+                    group_tokens(c - 1)
                 if hp == 1 and c > 0:
-                    feat_quant(2 * c - 1)
+                    quantize_dz(2 * c - 1)
                 if i == 2:
-                    for h in range(2):
-                        quantize(xc[:, 512 * h : 512 * h + 512], xs[:, 512 * h : 512 * h + 512], x_grp[h], E4)
+                    quantize_x(0)
                 if i >= 3:
-                    w_quant(i - 3, 0)
-                if hp == 0 and c + 1 < NCH:
-                    wd_int(scopy, c + 1, 0, 0, 512)
-                mul_p(i, 1)
-                for n in dws[2:3]:
-                    dw_copy(n)
-                if hp == 1 and c + 1 < NCH:
-                    wd_quant(c + 1, 0)
-                if more:
-                    acts_silu(i + 1)
-                mul_up(i)
-                for n in dws[3:4]:
-                    dw_copy(n)
-                for n in dws[4:6]:
-                    dw_pe(n)
+                    quantize_w(i - 3, 0)
+                if hp == 0 and 0 < c and next_chunk:
+                    group_wd(scalar_copy, c + 1, 0, 0, PASS)
+                make_p(i, 1)
+                if i == 2:
+                    quantize_x(1)
+                for n in blocks[2:3]:
+                    dw_out(n, scalar_copy)
+                if hp == 1 and next_chunk:
+                    quantize_wd(c + 1, 0)
+                if next_step:
+                    silu_minus(i + 1)
                 if i >= 2:
-                    w_int(scopy, i - 2, 0, vs, 512)
-                turn_pe(i, False)
-                mul_q(i)
-                for n in dws[4:5]:
-                    dw_copy(n)
-                turn_copy(i, False)
-                for n in dws[5:6]:
-                    dw_copy(n)
+                    group_w(vector_copy, i - 2, 0)
+                make_dz_up(i)
+                for n in blocks[3:4]:
+                    dw_out(n, scalar_copy)
+                for n in blocks[4:6]:
+                    dw(n)
+                if i >= 2:
+                    group_w(scalar_copy, i - 2, 0)
+                turn_dz(i, False)
+                make_q(i)
+                for n in blocks[4:5]:
+                    dw_out(n, scalar_copy)
+                if i == 0:
+                    group_wd(scalar_copy, 1, 0, 0, PASS)
+                copy_turned_dz(i, False)
+                if i == 0:
+                    group_wd(scalar_copy, 1, 1, V_COLS_WD_NEXT, PASS)
+                for n in blocks[5:6]:
+                    dw_out(n, scalar_copy)
                 if hp == 0 and c > 0:
-                    tok_quant(c - 1)
-                if hp == 1 and c + 1 < NCH:
-                    wd_quant(c + 1, 1)
-                if more:
-                    dh_j(i + 1, 0)
+                    quantize_tokens(c - 1)
+                if hp == 1 and next_chunk:
+                    quantize_wd(c + 1, 1)
+                if hp == 1 and not next_chunk:
+                    quantize_dz(2 * c - 2)
+                if next_step:
+                    dh_slot(i + 1, 0)
                 if i >= 4:
-                    dx(i - 4, range(4))
-                mul_gate(i)
-                if hp == 0 and c + 1 < NCH:
-                    wd_int(vcopy, c + 1, 1, 0, 512)
-                if hp == 1 and c > 0:
-                    feat_quant(2 * c - 2)
-                if i >= 2:
-                    w_int(vcopy, i - 2, 0, 0, vs)
+                    dx(i - 4, 0)
+                make_dz_gate(i)
+                if hp == 0 and next_chunk:
+                    group_wd(vector_copy, c + 1, 1, 0, V_COLS_WD_NEXT if c == 0 else PASS)
+                if hp == 1 and 0 < c and next_chunk:
+                    quantize_dz(2 * c - 2)
                 if i == 1:
-                    interleave(vcopy, x_grp[0], x_raw[0][:], 0, 512)
-                    interleave(scopy, x_grp[1], x_raw[1][:], 0, 512)
-            last = NCH - 1
-            flush_stores()
+                    group(scalar_copy, x_grouped[1], x_raw[1], 0, N)
+
+            last = CHUNKS - 1
+            issue_stores()
             for u in range(4, UNITS):
                 load_w(u, 1)
-            dwl = [(last - 1, 3, h) for h in range(2)] + [(last, b, h) for b in range(4) for h in range(2)]
-            dw_pe(dwl[0])
-            dw_pe(dwl[1])
-            turn_pe(STEPS - 1, True)
-            dx(4, range(4))
-            w_quant(5, 0)
-            dw_copy(dwl[0])
-            tok_int(last)
-            w_int(vcopy, 6, 0, 0, 256)
-            w_int(scopy, 6, 0, 256, 512)
-            turn_copy(STEPS - 1, True)
-            dw_copy(dwl[1])
-            flush_stores()
-            tok_quant(last)
-            dx(5, range(4))
-            w_int(vcopy, 7, 0, 0, 256)
-            w_int(scopy, 7, 0, 256, 512)
-            dw_pe(dwl[2])
-            dw_pe(dwl[3])
-            feat_quant(7)
-            feat_quant(6)
-            w_quant(6, 0)
-            dx(6, range(4))
-            w_int(scopy, 0, 1, 256, 512)
-            dw_copy(dwl[2])
-            w_int(vcopy, 0, 1, 0, 256)
-            w_quant(7, 0)
-            dx(7, range(4))
-            dw_copy(dwl[3])
-            flush_stores()
-            w_int(vcopy, 1, 1, 0, 256)
-            w_int(scopy, 1, 1, 256, 512)
-            dw_pe(dwl[4])
-            dw_pe(dwl[5])
-            w_quant(0, 1)
-            dn = 4
+            blocks = [(last - 1, 3, h) for h in range(2)] + [(last, b, h) for b in range(4) for h in range(2)]
+            dw(blocks[0])
+            dw(blocks[1])
+            turn_dz(STEPS - 1, True)
+            dx(4, 0)
+            quantize_w(5, 0)
+            dw_out(blocks[0], scalar_copy)
+            group_tokens(last)
+            group_w(vector_copy, 6, 0)
+            group_w(scalar_copy, 6, 0)
+            copy_turned_dz(STEPS - 1, True)
+            dw_out(blocks[1], scalar_copy)
+            issue_stores()
+            quantize_tokens(last)
+            dx(5, 0)
+            group_w(vector_copy, 7, 0)
+            group_w(scalar_copy, 7, 0)
+            dw(blocks[2])
+            dw(blocks[3])
+            quantize_dz(UNITS - 1)
+            quantize_dz(UNITS - 2)
+            quantize_w(6, 0)
+            dx(6, 0)
+            group_w(scalar_copy, 0, 1)
+            dw_out(blocks[2], scalar_copy)
+            group_w(vector_copy, 0, 1)
+            quantize_w(7, 0)
+            dx(7, 0)
+            dw_out(blocks[3], scalar_copy)
+            issue_stores()
+            group_w(vector_copy, 1, 1)
+            group_w(scalar_copy, 1, 1)
+            dw(blocks[4])
+            dw(blocks[5])
+            quantize_w(0, 1)
+
             for u in range(UNITS):
                 if u + 2 < UNITS:
-                    vs = (320, 320, 320, 320, 320, 320, 0, 0)[u]
-                    w_int(vcopy, u + 2, 1, 0, vs)
-                    w_int(scopy, u + 2, 1, vs, 512)
+                    group_w(vector_copy, u + 2, 1)
+                    group_w(scalar_copy, u + 2, 1)
                 if u < 2:
-                    dx_out(vcopy, 2 * u)
-                if u < 6:
-                    dw_copy(dwl[dn])
-                    if dn + 2 < 10:
-                        dw_pe(dwl[dn + 2])
-                    dn += 1
+                    dx_out(2 * u, vector_copy)
+                if u < 5:
+                    dw_out(blocks[4 + u], scalar_copy)
+                if u < 4:
+                    dw(blocks[6 + u])
                 if u < 2:
-                    dx_out(scopy, 2 * u + 1)
-                flush_stores()
+                    dx_out(2 * u + 1, scalar_copy)
+                issue_stores()
                 if u + 1 < UNITS:
-                    w_quant(u + 1, 1)
-                dx(u, range(4, 8))
-            for m in range(4, 8):
-                dx_out((vcopy, scopy)[m % 2], m)
+                    quantize_w(u + 1, 1)
+                if u == 5:
+                    dw_out(blocks[9], vector_copy)
+                dx(u, 1)
+            for m in range(SLOTS, 2 * SLOTS):
+                dx_out(m, (vector_copy, scalar_copy)[m % 2])

from contextlib import ExitStack

import concourse.mybir as mybir
from concourse.masks import make_identity

T, D, F = 512, 1024, 2048
FLOPS = 2 * T * D * F + 2 * T * (2 * F) * D + 2 * F * T * D

F32 = mybir.dt.float32
BF16 = mybir.dt.bfloat16
U32 = mybir.dt.uint32
U8 = mybir.dt.uint8
E4M3 = mybir.dt.float8_e4m3fn_x4
E5M2 = mybir.dt.float8_e5m2_x4
ACT = mybir.ActivationFunctionType
ALU = mybir.AluOpType
ENGINE = mybir.EngineType

P = 128
SLOTS = 4
PASS = P * SLOTS
N = 512
CHUNKS = F // PASS
STEPS = 2 * CHUNKS
UNITS = 2 * CHUNKS

DX_BANK = (0, 1, 2, 3, 4, 6, 0, 1)
DH_BANK = 4
TURN_BANK = 6
DW_BANKS = (5, 7)
DW_FIRST_STEP = 3

V_COLS_W = (
    (0, 128, 128, 128, 128, 128, 256, 256),
    (256, 256, 384, 384, 384, 320, 320, 256),
)
V_COLS_WD_HEAD = 192
V_COLS_WD_NEXT = 256


def tile_mixllamamlp_v_kernel(tc, x, W_gate, W_up, W_down, z_gate, z_up, grad_out, out_0, out_1):
    nc = tc.nc
    x_rows = x.flatten_outer_dims().rearrange("(p j) d -> p j d", j=SLOTS)
    g_rows = grad_out.flatten_outer_dims().rearrange("(p j) d -> p j d", j=SLOTS)
    dx_rows = out_0.flatten_outer_dims().rearrange("(p j) d -> p j d", j=SLOTS)
    zg_rows = z_gate.rearrange("(p j) f -> p j f", j=SLOTS)
    zu_rows = z_up.rearrange("(p j) f -> p j f", j=SLOTS)
    wd_rows = W_down.rearrange("(k p j) f -> k p j f", p=P, j=SLOTS)
    w_rows = [w.rearrange("(c p j) d -> c p j d", p=P, j=SLOTS) for w in (W_gate, W_up)]

    with ExitStack() as ctx:
        pool = ctx.enter_context(tc.tile_pool(name="sb", bufs=1))
        psum = ctx.enter_context(tc.psum_pool(name="ps", bufs=1))
        vector_copy = nc.vector.tensor_copy
        scalar_copy = nc.scalar.copy

        def sb(tag, shape, dtype, bufs):
            return pool.tile(shape, dtype, name=tag, tag=tag, bufs=bufs, align_bytes=64)

        def bank(k):
            return psum.tile([P, N], F32, name="bank%d" % k, tag="bank%d" % k, bufs=1)

        def raw_tile(shape):
            return sb("raw", shape, BF16, 10)

        def grouped_tile():
            return sb("grouped", [P, N, SLOTS], BF16, 11)

        def stage_tile(shape):
            return sb("stage", shape, F32, 5)

        identity = sb("identity", [P, P], F32, 1)
        warm = sb("warm", [P, 1], F32, 1)
        g_codes = sb("g_codes", [P, 2, T], U32, 1)
        g_scales = sb("g_scales", [P, 2, T], U8, 1)
        x_codes = sb("x_codes", [P, D], U32, 1)
        x_scales = sb("x_scales", [P, D], U8, 1)
        dz_codes = sb("dz_codes", [P, UNITS, T], U32, 1)
        dz_scales = sb("dz_scales", [P, UNITS, T], U8, 1)

        zg, zu, th, sm = {}, {}, {}, {}
        wd_raw, wd_grouped, wd_codes, wd_scales = {}, {}, {}, {}
        w_raw, w_grouped, w_codes, w_scales = {}, {}, {}, {}
        g_raw, x_raw = {}, {}
        dz_gate, dz_up, dz_grouped = {}, {}, {}
        tok_grouped, tok_codes, tok_scales = {}, {}, {}
        dh, turned, dx_sum, dw_sum, stages = {}, {}, {}, {}, {}
        stores = []

        def load_half_z(tiles, rows, tag, i):
            c, hp = divmod(i, 2)
            tiles[i] = sb(tag, [P, 2, PASS], F32, 4)
            nc.sync.dma_start(out=tiles[i][:], in_=rows[:, 2 * hp : 2 * hp + 2, c * PASS : (c + 1) * PASS])

        def load_z(i):
            load_half_z(zg, zg_rows, "zg", i)
            load_half_z(zu, zu_rows, "zu", i)

        def load_g(hp):
            g_raw[hp] = raw_tile([P, 2, D])
            nc.sync.dma_start(out=g_raw[hp][:], in_=g_rows[:, 2 * hp : 2 * hp + 2, :])

        def load_x(h):
            x_raw[h] = raw_tile([P, SLOTS, N])
            nc.sync.dma_start(out=x_raw[h][:], in_=x_rows[:, :, N * h : N * h + N])

        def load_wd(c, k):
            wd_raw[c, k] = raw_tile([P, SLOTS, PASS])
            nc.sync.dma_start(out=wd_raw[c, k][:], in_=wd_rows[k, :, :, c * PASS : (c + 1) * PASS])

        def load_w(u, h):
            w_raw[u, h] = raw_tile([P, SLOTS, N])
            nc.sync.dma_start(out=w_raw[u, h][:], in_=w_rows[u % 2][u // 2, :, :, N * h : N * h + N])

        def issue_stores():
            while stores:
                dst, src = stores.pop(0)
                nc.sync.dma_start(out=dst, in_=src)

        def group(copy, dst, raw, c0, c1):
            copy(
                out=dst[:, c0:c1, :].rearrange("p (c i) t -> p c t i", i=4),
                in_=raw[:, :, c0:c1].rearrange("p t (c i) -> p c t i", i=4),
            )

        def quantize(codes, scales, grouped, fmt):
            nc.vector.quantize_mx(out=codes.bitcast(fmt), scales=scales, in_=grouped[:].rearrange("p c t -> p (c t)"))

        def group_wd(copy, c, k, c0, c1):
            if (c, k) not in wd_grouped:
                wd_grouped[c, k] = grouped_tile()
            group(copy, wd_grouped[c, k], wd_raw[c, k], c0, c1)

        def quantize_wd(c, k):
            wd_codes[c, k] = sb("wd_codes", [P, PASS], U32, 4)
            wd_scales[c, k] = sb("wd_scales", [P, PASS], U8, 4)
            quantize(wd_codes[c, k][:], wd_scales[c, k][:], wd_grouped[c, k], E4M3)

        def group_w(copy, u, h):
            cut = V_COLS_W[h][u]
            c0, c1 = (0, cut) if copy is vector_copy else (cut, N)
            if c0 < c1:
                if (u, h) not in w_grouped:
                    w_grouped[u, h] = grouped_tile()
                group(copy, w_grouped[u, h], w_raw[u, h], c0, c1)

        def quantize_w(u, h):
            w_codes[u, h] = sb("w_codes", [P, N], U32, 5)
            w_scales[u, h] = sb("w_scales", [P, N], U8, 5)
            quantize(w_codes[u, h][:], w_scales[u, h][:], w_grouped[u, h], E4M3)

        def quantize_x(h):
            cols = slice(N * h, N * h + N)
            quantize(x_codes[:, cols], x_scales[:, cols], x_grouped[h], E4M3)

        def transpose_words(out, words, j0, w0):
            for jj in range(2):
                for u in range(2):
                    block = 2 * jj + u
                    nc.tensor.transpose(
                        out[:, block * P : (block + 1) * P], words[:, j0 + jj, w0 + u : w0 + 256 : 2], identity[:]
                    )

        def copy_turned(copy, dst, src, hp):
            copy(
                out=dst[:].bitcast(F32)[:, 256 * hp : 256 * hp + 256, :].rearrange("p (jj r) u -> p jj r u", jj=2),
                in_=src[:].rearrange("p (jj u r) -> p jj r u", jj=2, u=2),
            )

        def turn_dz(i, gate):
            c, hp = divmod(i, 2)
            turned[i, gate] = bank(TURN_BANK)
            if gate:
                transpose_words(turned[i, gate], dz_gate[c][:].bitcast(F32), 2 * hp, 0)
            else:
                transpose_words(turned[i, gate], dz_up[i][:].bitcast(F32), 0, 0)

        def copy_turned_dz(i, gate):
            c, hp = divmod(i, 2)
            u = 2 * c if gate else 2 * c + 1
            if hp == 0:
                dz_grouped[u] = grouped_tile()
            copy_turned(scalar_copy, dz_grouped[u], turned[i, gate], hp)

        def quantize_dz(u):
            quantize(dz_codes[:, u, :], dz_scales[:, u, :], dz_grouped[u], E5M2)

        def dh_slot(i, jj):
            c, hp = divmod(i, 2)
            dh[i, jj] = bank(DW_BANKS[0] if jj == 1 and i < DW_FIRST_STEP else DH_BANK)
            j = 2 * hp + jj
            cols = slice(j * P, (j + 1) * P)
            for k in range(2):
                nc.tensor.matmul_mx(
                    out=dh[i, jj][:],
                    lhsT=g_codes[:, k, cols].bitcast(E5M2),
                    lhsT_scale=g_scales[:, k, cols],
                    rhs=wd_codes[c, k][:].bitcast(E4M3),
                    rhs_scale=wd_scales[c, k][:],
                    start=(k == 0),
                    stop=(k == 1),
                )

        def tanh_half(i):
            th[i] = sb("th", [P, 2, PASS], F32, 3)
            nc.scalar.activation(out=th[i][:], in_=zg[i][:], func=ACT.Tanh, scale=0.5)

        def silu_minus(i):
            sm[i] = sb("sm", [P, 2, PASS], F32, 3)
            nc.scalar.activation(out=sm[i][:], in_=zg[i][:], func=ACT.Silu, scale=-1.0)

        def times(out, a, scalar, b, op):
            nc.vector.scalar_tensor_tensor(out=out, in0=a, scalar=scalar, in1=b, op0=op, op1=ALU.mult)

        def make_p(i, jj):
            times(th[i][:, jj, :], th[i][:, jj, :], 1.0, dh[i, jj][:], ALU.add)

        def make_dz_up(i):
            dz_up[i] = sb("dz_up", [P, 2, PASS], BF16, 2)
            times(dz_up[i][:], th[i][:], 0.5, zg[i][:], ALU.mult)

        def make_q(i):
            times(zu[i][:], th[i][:], -0.5, zu[i][:], ALU.mult)

        def make_dz_gate(i):
            c, hp = divmod(i, 2)
            if hp == 0:
                dz_gate[c] = sb("dz_gate", [P, SLOTS, PASS], BF16, 2)
            times(dz_gate[c][:, 2 * hp : 2 * hp + 2, :], sm[i][:], 1.0, zu[i][:], ALU.subtract)

        def group_tokens(c):
            tok_grouped[c] = grouped_tile()
            group(vector_copy, tok_grouped[c], dz_gate[c], 0, PASS)

        def quantize_tokens(c):
            tok_codes[c] = sb("tok_codes", [P, PASS], U32, 2)
            tok_scales[c] = sb("tok_scales", [P, PASS], U8, 2)
            quantize(tok_codes[c][:], tok_scales[c][:], tok_grouped[c], E5M2)

        def dw(n):
            c, b, h = n
            dw_sum[n] = bank(DW_BANKS[h])
            rows, cols = slice(b * P, (b + 1) * P), slice(N * h, N * h + N)
            nc.tensor.matmul_mx(
                out=dw_sum[n][:],
                lhsT=tok_codes[c][:, rows].bitcast(E5M2),
                lhsT_scale=tok_scales[c][:, rows],
                rhs=x_codes[:, cols].bitcast(E4M3),
                rhs_scale=x_scales[:, cols],
                start=True,
                stop=True,
            )

        def dw_out(n, copy):
            c, b, h = n
            if h == 0:
                stages[c, b] = stage_tile([P, D])
            copy(out=stages[c, b][:, N * h : N * h + N], in_=dw_sum[n][:])
            if h == 1:
                row = c * PASS + b * P
                stores.append((out_1[row : row + P, :], stages[c, b][:]))

        def dx(u, h):
            for j in range(SLOTS):
                m = SLOTS * h + j
                cols = slice(j * P, (j + 1) * P)
                if u == 0:
                    dx_sum[m] = bank(DX_BANK[m])
                nc.tensor.matmul_mx(
                    out=dx_sum[m][:],
                    lhsT=dz_codes[:, u, cols].bitcast(E5M2),
                    lhsT_scale=dz_scales[:, u, cols],
                    rhs=w_codes[u, h][:].bitcast(E4M3),
                    rhs_scale=w_scales[u, h][:],
                    start=(u == 0),
                    stop=(u == UNITS - 1),
                )

        def dx_out(m, copy):
            h, j = divmod(m, SLOTS)
            if j % 2 == 0:
                stages["dx", m] = stage_tile([P, 2, N])
            half_stage = stages["dx", m - j % 2][:, j % 2, :]
            copy(out=half_stage, in_=dx_sum[m][:])
            nc.sync.dma_start(out=dx_rows[:, j, N * h : N * h + N], in_=half_stage)

        with tc.manual_schedule(engines={ENGINE.DVE, ENGINE.Activation, ENGINE.SP}):
            make_identity(nc, identity[:])
            nc.vector.memset(warm[:], 0.0)
            nc.scalar.activation(out=warm[:], in_=warm[:], func=ACT.Silu)

            load_wd(0, 0)
            load_g(0)
            load_g(1)
            load_wd(0, 1)
            load_half_z(zg, zg_rows, "zg", 0)
            load_x(0)
            load_half_z(zu, zu_rows, "zu", 0)
            load_z(1)
            load_wd(1, 0)
            load_wd(1, 1)
            load_z(2)
            load_x(1)

            group_wd(vector_copy, 0, 0, 0, PASS)
            quantize_wd(0, 0)
            g_grouped = [grouped_tile(), grouped_tile()]
            for hp in range(2):
                for k in range(2):
                    g_turned = bank((DH_BANK, TURN_BANK)[k])
                    transpose_words(g_turned, g_raw[hp][:].bitcast(F32), 0, 256 * k)
                    copy_turned((scalar_copy, vector_copy)[k], g_grouped[k], g_turned, hp)
            group_wd(vector_copy, 0, 1, 0, V_COLS_WD_HEAD)
            group_wd(scalar_copy, 0, 1, V_COLS_WD_HEAD, PASS)
            for k in range(2):
                quantize(g_codes[:, k, :], g_scales[:, k, :], g_grouped[k], E5M2)
            quantize_wd(0, 1)
            dh_slot(0, 0)
            tanh_half(0)
            silu_minus(0)
            x_grouped = [grouped_tile(), grouped_tile()]
            group(vector_copy, x_grouped[0], x_raw[0], 0, N)

            for i in range(STEPS):
                c, hp = divmod(i, 2)
                next_step = i + 1 < STEPS
                next_chunk = c + 1 < CHUNKS

                if i == 0:
                    load_wd(2, 0)
                    load_wd(2, 1)
                    load_z(3)
                if 1 < i and i + 2 < STEPS:
                    load_z(i + 2)
                load_w(i, 0)
                if hp == 0 and 0 < c and c + 2 < CHUNKS:
                    load_wd(c + 2, 0)
                    load_wd(c + 2, 1)
                if i >= 4:
                    load_w(i - 4, 1)
                issue_stores()

                if hp == 1:
                    blocks = [(c - 1, b, h) for b in range(3) for h in range(2)] if c > 0 else []
                else:
                    blocks = [(c - 2, 3, h) for h in range(2)] if c > 1 else []

                for n in blocks[0:2]:
                    dw(n)
                if i > 0:
                    turn_dz(i - 1, True)
                make_p(i, 0)
                dh_slot(i, 1)
                for n in blocks[0:1]:
                    dw_out(n, scalar_copy)
                if next_step:
                    tanh_half(i + 1)
                if i > 0:
                    copy_turned_dz(i - 1, True)
                for n in blocks[1:2]:
                    dw_out(n, scalar_copy)
                for n in blocks[2:4]:
                    dw(n)
                if hp == 0 and c > 0:
                    group_tokens(c - 1)
                if hp == 1 and c > 0:
                    quantize_dz(2 * c - 1)
                if i == 2:
                    quantize_x(0)
                if i >= 3:
                    quantize_w(i - 3, 0)
                if hp == 0 and 0 < c and next_chunk:
                    group_wd(scalar_copy, c + 1, 0, 0, PASS)
                make_p(i, 1)
                if i == 2:
                    quantize_x(1)
                for n in blocks[2:3]:
                    dw_out(n, scalar_copy)
                if hp == 1 and next_chunk:
                    quantize_wd(c + 1, 0)
                if next_step:
                    silu_minus(i + 1)
                if i >= 2:
                    group_w(vector_copy, i - 2, 0)
                make_dz_up(i)
                for n in blocks[3:4]:
                    dw_out(n, scalar_copy)
                for n in blocks[4:6]:
                    dw(n)
                if i >= 2:
                    group_w(scalar_copy, i - 2, 0)
                turn_dz(i, False)
                make_q(i)
                for n in blocks[4:5]:
                    dw_out(n, scalar_copy)
                if i == 0:
                    group_wd(scalar_copy, 1, 0, 0, PASS)
                copy_turned_dz(i, False)
                if i == 0:
                    group_wd(scalar_copy, 1, 1, V_COLS_WD_NEXT, PASS)
                for n in blocks[5:6]:
                    dw_out(n, scalar_copy)
                if hp == 0 and c > 0:
                    quantize_tokens(c - 1)
                if hp == 1 and next_chunk:
                    quantize_wd(c + 1, 1)
                if hp == 1 and not next_chunk:
                    quantize_dz(2 * c - 2)
                if next_step:
                    dh_slot(i + 1, 0)
                if i >= 4:
                    dx(i - 4, 0)
                make_dz_gate(i)
                if hp == 0 and next_chunk:
                    group_wd(vector_copy, c + 1, 1, 0, V_COLS_WD_NEXT if c == 0 else PASS)
                if hp == 1 and 0 < c and next_chunk:
                    quantize_dz(2 * c - 2)
                if i == 1:
                    group(scalar_copy, x_grouped[1], x_raw[1], 0, N)

            last = CHUNKS - 1
            issue_stores()
            for u in range(4, UNITS):
                load_w(u, 1)
            blocks = [(last - 1, 3, h) for h in range(2)] + [(last, b, h) for b in range(4) for h in range(2)]
            dw(blocks[0])
            dw(blocks[1])
            turn_dz(STEPS - 1, True)
            dx(4, 0)
            quantize_w(5, 0)
            dw_out(blocks[0], scalar_copy)
            group_tokens(last)
            group_w(vector_copy, 6, 0)
            group_w(scalar_copy, 6, 0)
            copy_turned_dz(STEPS - 1, True)
            dw_out(blocks[1], scalar_copy)
            issue_stores()
            quantize_tokens(last)
            dx(5, 0)
            group_w(vector_copy, 7, 0)
            group_w(scalar_copy, 7, 0)
            dw(blocks[2])
            dw(blocks[3])
            quantize_dz(UNITS - 1)
            quantize_dz(UNITS - 2)
            quantize_w(6, 0)
            dx(6, 0)
            group_w(scalar_copy, 0, 1)
            dw_out(blocks[2], scalar_copy)
            group_w(vector_copy, 0, 1)
            quantize_w(7, 0)
            dx(7, 0)
            dw_out(blocks[3], scalar_copy)
            issue_stores()
            group_w(vector_copy, 1, 1)
            group_w(scalar_copy, 1, 1)
            dw(blocks[4])
            dw(blocks[5])
            quantize_w(0, 1)

            for u in range(UNITS):
                if u + 2 < UNITS:
                    group_w(vector_copy, u + 2, 1)
                    group_w(scalar_copy, u + 2, 1)
                if u < 2:
                    dx_out(2 * u, vector_copy)
                if u < 5:
                    dw_out(blocks[4 + u], scalar_copy)
                if u < 4:
                    dw(blocks[6 + u])
                if u < 2:
                    dx_out(2 * u + 1, scalar_copy)
                issue_stores()
                if u + 1 < UNITS:
                    quantize_w(u + 1, 1)
                if u == 5:
                    dw_out(blocks[9], vector_copy)
                dx(u, 1)
            for m in range(SLOTS, 2 * SLOTS):
                dx_out(m, (vector_copy, scalar_copy)[m % 2])
